import numpy as np
import ml_dtypes


def mxq(x, axis, fmt="e4m3"):
    dtype, down = {"e4m3": (ml_dtypes.float8_e4m3fn, 7), "e5m2": (ml_dtypes.float8_e5m2, 14)}[fmt]
    v = np.moveaxis(np.asarray(x, np.float32).astype(ml_dtypes.bfloat16).astype(np.float64), axis, -1)
    blocks = v.reshape(v.shape[:-1] + (-1, 32))
    amax = np.abs(blocks).max(-1, keepdims=True)
    byte = np.maximum(np.where(amax > 0, np.frexp(amax)[1] - 1 + 127, 0) - down, 1)
    scale = np.exp2(byte - 127.0)
    codes = (blocks / scale).astype(np.float32).astype(dtype).astype(np.float64)
    return np.moveaxis((codes * scale).reshape(v.shape), -1, axis)


WIDE = False


def mx_kscale(k):
    if not WIDE:
        return np.ones(k)
    levels = np.array([10, -10, 5, -5, 0])
    a = np.random.permutation(np.resize(levels, k // 512 * 4)).reshape(k // 512, 4)
    idx = np.arange(k)
    return np.exp2(a[idx // 512, idx % 128 // 32])


BF16 = ml_dtypes.bfloat16


def bf(x):
    return np.asarray(x, np.float32).astype(BF16)


def f64(x):
    return np.asarray(x).astype(np.float64)


E2M1 = np.array([0.0, 0.5, 1.0, 1.5, 2.0, 3.0, 4.0, 6.0, -0.0, -0.5, -1.0, -1.5, -2.0, -3.0, -4.0, -6.0])


def pack_weight(w, fmt):
    k, n = w.shape
    w = f64(bf(w)).reshape(k // 32, 32, n)
    amax = np.abs(w).max(1)
    if fmt == "e4m3":
        byte = np.frexp(amax)[1] - 1 + 127 - 7
    else:
        mant, ex = np.frexp(amax / 6.0)
        byte = np.where(mant > 0.5, ex, ex - 1) + 127
    byte = np.clip(np.where(amax > 0, byte, 1), 1, 254)
    scaled = (w * np.exp2(127.0 - byte)[:, None, :]).reshape(k, n).astype(np.float32)
    by_word = np.ascontiguousarray(scaled.reshape(k // 512, 128, 4, n).transpose(0, 1, 3, 2))
    if fmt == "e4m3":
        words = by_word.astype(ml_dtypes.float8_e4m3fn).view(np.uint8)
    else:
        c = by_word.astype(ml_dtypes.float4_e2m1fn).view(np.uint8) & 0xF
        words = c[..., 0::2] | (c[..., 1::2] << 4)
    return np.ascontiguousarray(words), np.ascontiguousarray(byte.astype(np.uint8).reshape(k // 512, 16, n))


def unpack_weight(words, scales, fmt):
    g, p, n, _ = words.shape
    if fmt == "e4m3":
        vals = np.ascontiguousarray(words).view(ml_dtypes.float8_e4m3fn).astype(np.float64)
    else:
        nib = np.empty((g, p, n, 4), np.uint8)
        nib[..., 0::2] = words & 0xF
        nib[..., 1::2] = words >> 4
        vals = E2M1[nib]
    vals = vals * np.repeat(np.exp2(scales.astype(np.float64) - 127.0), 8, axis=1)[..., None]
    return vals.transpose(0, 1, 3, 2).reshape(g * 512, n)


B, N, HD, ED, F = 1, 32, 256, 512, 1024
TD = HD + HD
MD = TD + ED
EPS = 1e-5
FMT = "e4m3"


def layer_norm(x, g, b):
    mu = x.mean(-1, keepdims=True)
    var = x.var(-1, keepdims=True)
    return (x - mu) * (1.0 / np.sqrt(var + EPS)) * g + b


def setup_inputs():
    t = mx_kscale(F)
    rx = mx_kscale(MD)[:HD]
    r = np.concatenate([rx, rx, np.ones(ED)])
    hid = bf(np.maximum(np.random.standard_normal((B, N, N, F)), 0.0) * t)
    x_down = bf(np.random.standard_normal((B, N, HD)) * rx)
    p_ln = bf(np.random.standard_normal((B, N, N, ED)))
    W2_words, W2_scales = pack_weight(np.random.standard_normal((F, MD)) / np.sqrt(F) / t[:, None] * r, FMT)
    b2 = bf(0.1 * np.random.standard_normal(MD) * r)
    Wo_words, Wo_scales = pack_weight(np.random.standard_normal((MD, ED)) / np.sqrt(MD) / r[:, None], FMT)
    bo = bf(0.1 * np.random.standard_normal(ED))
    ln_out_g = bf(1.0 + 0.1 * np.random.standard_normal(ED))
    ln_out_b = bf(0.1 * np.random.standard_normal(ED))
    return {"hid": hid,
            "x_down": x_down,
            "p_ln": p_ln,
            "W2_words": W2_words,
            "W2_scales": W2_scales,
            "b2": b2,
            "Wo_words": Wo_words,
            "Wo_scales": Wo_scales,
            "bo": bo,
            "ln_out_g": ln_out_g,
            "ln_out_b": ln_out_b}


def reference(hid, x_down, p_ln, W2_words, W2_scales, b2, Wo_words, Wo_scales, bo, ln_out_g, ln_out_b):
    xd, pl = f64(x_down), f64(p_ln)
    edge_bias = np.concatenate([np.broadcast_to(xd[:, :, None, :], (B, N, N, HD)),
                                np.broadcast_to(xd[:, None, :, :], (B, N, N, HD))], axis=-1)
    z_in = np.concatenate([edge_bias, pl], axis=-1)
    m = np.maximum((mxq(f64(hid), 3, "e4m3") @ unpack_weight(W2_words, W2_scales, FMT)) + f64(b2), 0.0)
    z = (mxq(m + z_in, 3, "e4m3") @ unpack_weight(Wo_words, Wo_scales, FMT)) + f64(bo)
    return pl + layer_norm(z, f64(ln_out_g), f64(ln_out_b))

@@ -1,0 +1,257 @@
+from contextlib import ExitStack
+
+import concourse.mybir as mybir
+from concourse.masks import make_identity
+
+F32 = mybir.dt.float32
+BF16 = mybir.dt.bfloat16
+I32 = mybir.dt.int32
+U32 = mybir.dt.uint32
+U8 = mybir.dt.uint8
+FP8X4 = mybir.dt.float8_e4m3fn_x4
+ALU = mybir.AluOpType
+ACT = mybir.ActivationFunctionType
+
+P = 128
+NODES = 32
+EDGES = NODES * NODES
+TILES = EDGES // P
+HD = 256
+ED = 512
+F = 1024
+MD = 1024
+GROUPS = 2
+BANK = 512
+EPS = 1e-5
+
+FLOPS = 2 * EDGES * F * MD + 2 * EDGES * MD * ED
+
+
+def tile_edgeupdaterwrapper_v01_pb_kernel(
+    tc, hid, x_down, p_ln, W2_words, W2_scales, b2, Wo_words, Wo_scales, bo, ln_out_g, ln_out_b, out
+):
+    nc = tc.nc
+
+    hid_rows = hid.flatten_outer_dims().rearrange("(p r) f -> p r f", r=TILES)
+    p_ln_rows = p_ln.flatten_outer_dims().rearrange("(p r) f -> p r f", r=TILES)
+    out_rows = out.flatten_outer_dims().rearrange("(p r) f -> p r f", r=TILES)
+    nodes = x_down.flatten_outer_dims()
+
+    with ExitStack() as ctx:
+        ctx.enter_context(tc.manual_schedule())
+        keep = ctx.enter_context(tc.tile_pool(name="keep", bufs=1))
+        work = ctx.enter_context(tc.tile_pool(name="work", bufs=3))
+        stats = ctx.enter_context(tc.tile_pool(name="stats", bufs=4))
+        psum_t = ctx.enter_context(tc.psum_pool(name="psum_t", bufs=2))
+        psum_y = ctx.enter_context(tc.psum_pool(name="psum_y", bufs=4))
+        psum_z = ctx.enter_context(tc.psum_pool(name="psum_z", bufs=2))
+
+        hid_sb = keep.tile([P, TILES, F], BF16)
+        node_i = keep.tile([P, HD], BF16)
+        z_rest = keep.tile([P, TILES, MD - HD], BF16)
+        w2_sb = keep.tile([P, GROUPS, 4 * MD], U8, align_bytes=64)
+        wo_sb = keep.tile([P, GROUPS, 4 * ED], U8, align_bytes=64)
+        planes = keep.tile([P, MD], U8, align_bytes=64)
+        b2_bc = keep.tile([P, MD], BF16)
+        bo_bc = keep.tile([P, ED], BF16)
+        g_bc = keep.tile([P, ED], BF16)
+        lnb_bc = keep.tile([P, ED], BF16)
+        resid = keep.tile([P, TILES, ED], F32)
+        ident = keep.tile([P, P], F32)
+        eps = keep.tile([P, 1], F32)
+        hid_codes = keep.tile([P, TILES, GROUPS, P], U32, align_bytes=64)
+        hid_scales = keep.tile([P, TILES, GROUPS, P], U8, align_bytes=64)
+
+        nc.vector.memset(planes[:].bitcast(I32), 0)
+        nc.vector.memset(eps[:], EPS)
+        make_identity(nc, ident[:])
+
+        def load_hid(first, count):
+            nc.sync.dma_start(out=hid_sb[:, first : first + count, :], in_=hid_rows[:, first : first + count, :])
+
+        def load_p_ln(first, count):
+            nc.sync.dma_start(
+                out=z_rest[:, first : first + count, HD : MD - HD], in_=p_ln_rows[:, first : first + count, :]
+            )
+
+        def load_planes(scales, first_row, width):
+            for q in range(4):
+                nc.sync.dma_start(
+                    out=planes[32 * q + first_row : 32 * q + first_row + 8, 0:width].bitcast(I32),
+                    in_=scales[:, 4 * q : 4 * q + 4, :].bitcast(I32),
+                )
+
+        load_hid(0, 2)
+        load_planes(W2_scales, 0, MD)
+        for h in range(MD // BANK):
+            nc.sync.dma_start(
+                out=w2_sb[:, :, 4 * BANK * h : 4 * BANK * (h + 1)].bitcast(I32),
+                in_=W2_words[:, :, BANK * h : BANK * (h + 1), :].rearrange("g p n t -> p g (n t)").bitcast(I32),
+            )
+        nc.sync.dma_start(out=b2_bc[:], in_=b2.partition_broadcast(P))
+        nc.sync.dma_start(out=node_i[:], in_=nodes.unsqueeze(1).to_broadcast([NODES, 4, HD]))
+        for a in range(4):
+            nc.sync.dma_start(
+                out=z_rest[a:P:4, :, 0:HD],
+                in_=nodes[TILES * a : TILES * (a + 1), :].unsqueeze(0).to_broadcast([NODES, TILES, HD]),
+            )
+        load_p_ln(0, 2)
+        load_hid(2, 2)
+        load_planes(Wo_scales, 8, ED)
+        nc.sync.dma_start(
+            out=wo_sb[:].bitcast(I32), in_=Wo_words.rearrange("g p n t -> p g (n t)").bitcast(I32)
+        )
+        nc.sync.dma_start(out=bo_bc[:], in_=bo.partition_broadcast(P))
+        load_p_ln(2, 2)
+        load_hid(4, 2)
+        nc.sync.dma_start(out=g_bc[:], in_=ln_out_g.partition_broadcast(P))
+        nc.sync.dma_start(out=lnb_bc[:], in_=ln_out_b.partition_broadcast(P))
+        load_hid(6, 2)
+        load_p_ln(4, 4)
+
+        def to_k_on_partitions(rows_bf16, grouped):
+            words = rows_bf16.bitcast(F32)
+            turned = psum_t.tile([P, GROUPS, 2, P], F32)
+            for g in range(GROUPS):
+                for u in range(2):
+                    nc.tensor.transpose(turned[:, g, u, :], words[:, 256 * g + u : 256 * (g + 1) : 2], ident[:])
+            nc.scalar.copy(
+                out=grouped[:].bitcast(F32).rearrange("p (g e u) -> p g e u", g=GROUPS, u=2),
+                in_=turned[:].rearrange("p g u e -> p g e u"),
+            )
+
+        def quantise(grouped, codes, scales):
+            nc.vector.quantize_mx(
+                out=codes.rearrange("p g e -> p (g e)").bitcast(FP8X4),
+                scales=scales.rearrange("p g e -> p (g e)"),
+                in_=grouped[:],
+            )
+
+        live = {}
+
+        def turn_hid(r):
+            hid_grouped = work.tile([P, GROUPS * P * 4], BF16, align_bytes=64)
+            to_k_on_partitions(hid_sb[:, r, :], hid_grouped)
+            live["hid_grouped", r] = hid_grouped
+
+        def quantise_hid(r):
+            quantise(live["hid_grouped", r], hid_codes[:, r], hid_scales[:, r])
+
+        def first_matmul(r):
+            for h in range(MD // BANK):
+                y = psum_y.tile([P, BANK], F32)
+                for g in range(GROUPS):
+                    nc.tensor.matmul_mx(
+                        out=y[:],
+                        lhsT=hid_codes[:, r, g, :].bitcast(FP8X4),
+                        lhsT_scale=hid_scales[:, r, g, :],
+                        rhs=w2_sb[:, g, 4 * BANK * h : 4 * BANK * (h + 1)].bitcast(FP8X4),
+                        rhs_scale=planes[4 * g : P, BANK * h : BANK * (h + 1)],
+                        start=(g == 0),
+                        stop=(g == GROUPS - 1),
+                    )
+                live["y", r, h] = y
+
+        def add_b2(r):
+            pre = work.tile([P, MD], F32)
+            for h in range(MD // BANK):
+                cols = slice(BANK * h, BANK * (h + 1))
+                nc.vector.tensor_tensor(out=pre[:, cols], in0=live["y", r, h][:], in1=b2_bc[:, cols], op=ALU.add)
+            live["pre", r] = pre
+
+        def relu_add_z(r):
+            pre = live["pre", r]
+            s_sb = work.tile([P, MD], BF16)
+            nc.vector.scalar_tensor_tensor(
+                out=s_sb[:, 0:HD], in0=pre[:, 0:HD], scalar=0.0, in1=node_i[:], op0=ALU.max, op1=ALU.add
+            )
+            nc.vector.scalar_tensor_tensor(
+                out=s_sb[:, HD:MD], in0=pre[:, HD:MD], scalar=0.0, in1=z_rest[:, r, :], op0=ALU.max, op1=ALU.add
+            )
+            live["s", r] = s_sb
+
+        def turn_s(r):
+            s_grouped = work.tile([P, GROUPS * P * 4], BF16, align_bytes=64)
+            to_k_on_partitions(live["s", r][:], s_grouped)
+            live["s_grouped", r] = s_grouped
+
+        def quantise_s(r):
+            s_codes = work.tile([P, GROUPS, P], U32, align_bytes=64)
+            s_scales = work.tile([P, GROUPS, P], U8, align_bytes=64)
+            quantise(live["s_grouped", r], s_codes[:], s_scales[:])
+            live["s_codes", r] = s_codes
+            live["s_scales", r] = s_scales
+
+        def second_matmul(r):
+            acc = psum_z.tile([P, ED], F32)
+            for g in range(GROUPS):
+                nc.tensor.matmul_mx(
+                    out=acc[:],
+                    lhsT=live["s_codes", r][:, g, :].bitcast(FP8X4),
+                    lhsT_scale=live["s_scales", r][:, g, :],
+                    rhs=wo_sb[:, g, :].bitcast(FP8X4),
+                    rhs_scale=planes[8 + 4 * g : P, 0:ED],
+                    start=(g == 0),
+                    stop=(g == GROUPS - 1),
+                )
+            live["acc", r] = acc
+
+        def add_bo(r):
+            z = work.tile([P, ED], F32)
+            z_sum = stats.tile([P, 1], F32)
+            nc.vector.scalar_tensor_tensor(
+                out=z[:], in0=live["acc", r][:], scalar=1.0, in1=bo_bc[:], op0=ALU.mult, op1=ALU.add, accum_out=z_sum[:]
+            )
+            live["z", r] = z
+            live["z_sum", r] = z_sum
+
+        def variance(r):
+            neg_mean = stats.tile([P, 1], F32)
+            nc.vector.tensor_scalar_mul(out=neg_mean[:], in0=live["z_sum", r][:], scalar1=-1.0 / ED)
+            squares = work.tile([P, ED], F32)
+            sq_sum = stats.tile([P, 1], F32)
+            nc.scalar.activation(
+                out=squares[:], in_=live["z", r][:], func=ACT.Square, bias=neg_mean[:], scale=1.0, accum_out=sq_sum[:]
+            )
+            std = stats.tile([P, 1], F32)
+            nc.scalar.activation(out=std[:], in_=sq_sum[:], func=ACT.Sqrt, bias=eps[:], scale=1.0 / ED)
+            live["neg_mean", r] = neg_mean
+            live["std", r] = std
+
+        def centre_times_g(r):
+            scaled = work.tile([P, ED], F32)
+            nc.vector.scalar_tensor_tensor(
+                out=scaled[:], in0=live["z", r][:], scalar=live["neg_mean", r][:], in1=g_bc[:], op0=ALU.add, op1=ALU.mult
+            )
+            live["scaled", r] = scaled
+
+        def residual(r):
+            nc.gpsimd.tensor_tensor(out=resid[:, r, :], in0=z_rest[:, r, HD : MD - HD], in1=lnb_bc[:], op=ALU.add)
+
+        def finish(r):
+            rstd = stats.tile([P, 1], F32)
+            nc.vector.reciprocal(out=rstd[:], in_=live["std", r][:])
+            normed = work.tile([P, ED], F32)
+            nc.scalar.activation(out=normed[:], in_=live["scaled", r][:], func=ACT.Copy, scale=rstd[:])
+            result = work.tile([P, ED], F32)
+            nc.gpsimd.tensor_tensor(out=result[:], in0=normed[:], in1=resid[:, r, :], op=ALU.add)
+            nc.sync.dma_start(out=out_rows[:, r, :], in_=result[:])
+
+        def stage(work_of, r):
+            if 0 <= r < TILES:
+                work_of(r)
+
+        for k in range(-3, TILES + 2):
+            stage(first_matmul, k + 1)
+            stage(add_b2, k)
+            stage(quantise_s, k - 1)
+            stage(second_matmul, k - 1)
+            stage(relu_add_z, k)
+            stage(turn_s, k)
+            stage(add_bo, k - 1)
+            stage(quantise_hid, k + 2)
+            stage(variance, k - 1)
+            stage(residual, k)
+            stage(finish, k - 2)
+            stage(centre_times_g, k - 1)
+            stage(turn_hid, k + 3)

@@ -52,6 +52,11 @@ def tile_edgeupdaterwrapper_v01_pb_kernel(
         w2_sb = keep.tile([P, GROUPS, 4 * MD], U8, align_bytes=64)
         wo_sb = keep.tile([P, GROUPS, 4 * ED], U8, align_bytes=64)
         planes = keep.tile([P, MD], U8, align_bytes=64)
+        rows = keep.tile([P, MD], BF16)
+        node_rows = keep.tile([P, HD], BF16)
+        ident_bf = keep.tile([P, P], BF16)
+        pick_i = keep.tile([P, P], BF16)
+        pick_j = keep.tile([P, TILES, P], BF16)
         b2_bc = keep.tile([P, MD], BF16)
         bo_bc = keep.tile([P, ED], BF16)
         g_bc = keep.tile([P, ED], BF16)
@@ -64,7 +69,18 @@ def tile_edgeupdaterwrapper_v01_pb_kernel(
 
         nc.vector.memset(planes[:].bitcast(I32), 0)
         nc.vector.memset(eps[:], EPS)
+        nc.vector.memset(rows[:], 0.0)
+        nc.vector.memset(node_rows[:], 0.0)
         make_identity(nc, ident[:])
+        make_identity(nc, ident_bf[:])
+        nc.vector.tensor_copy(
+            out=pick_i[:].rearrange("k (q a) -> k q a", a=4),
+            in_=ident_bf[:, 0:NODES].unsqueeze(2).to_broadcast([P, NODES, 4]),
+        )
+        nc.vector.tensor_copy(
+            out=pick_j[:].rearrange("k r (q a) -> k r q a", a=4),
+            in_=ident_bf[:, 0:NODES].rearrange("k (a r) -> k r a", r=TILES).unsqueeze(2).to_broadcast([P, TILES, NODES, 4]),
+        )
 
         def load_hid(first, count):
             nc.sync.dma_start(out=hid_sb[:, first : first + count, :], in_=hid_rows[:, first : first + count, :])
@@ -81,6 +97,8 @@ def tile_edgeupdaterwrapper_v01_pb_kernel(
                     in_=scales[:, 4 * q : 4 * q + 4, :].bitcast(I32),
                 )
 
+        nc.sync.dma_start(out=node_rows[0:NODES, :], in_=nodes)
+        nc.sync.dma_start(out=rows[0:1, :], in_=b2.unsqueeze(0))
         load_hid(0, 2)
         load_planes(W2_scales, 0, MD)
         for h in range(MD // BANK):
@@ -88,26 +106,31 @@ def tile_edgeupdaterwrapper_v01_pb_kernel(
                 out=w2_sb[:, :, 4 * BANK * h : 4 * BANK * (h + 1)].bitcast(I32),
                 in_=W2_words[:, :, BANK * h : BANK * (h + 1), :].rearrange("g p n t -> p g (n t)").bitcast(I32),
             )
-        nc.sync.dma_start(out=b2_bc[:], in_=b2.partition_broadcast(P))
-        nc.sync.dma_start(out=node_i[:], in_=nodes.unsqueeze(1).to_broadcast([NODES, 4, HD]))
-        for a in range(4):
-            nc.sync.dma_start(
-                out=z_rest[a:P:4, :, 0:HD],
-                in_=nodes[TILES * a : TILES * (a + 1), :].unsqueeze(0).to_broadcast([NODES, TILES, HD]),
-            )
+        nc.sync.dma_start(out=rows[1:2, 0:ED], in_=bo.unsqueeze(0))
+        nc.sync.dma_start(out=rows[1:2, ED : 2 * ED], in_=ln_out_g.unsqueeze(0))
+        nc.sync.dma_start(out=rows[2:3, 0:ED], in_=ln_out_b.unsqueeze(0))
         load_p_ln(0, 2)
         load_hid(2, 2)
         load_planes(Wo_scales, 8, ED)
         nc.sync.dma_start(
             out=wo_sb[:].bitcast(I32), in_=Wo_words.rearrange("g p n t -> p g (n t)").bitcast(I32)
         )
-        nc.sync.dma_start(out=bo_bc[:], in_=bo.partition_broadcast(P))
         load_p_ln(2, 2)
         load_hid(4, 2)
-        nc.sync.dma_start(out=g_bc[:], in_=ln_out_g.partition_broadcast(P))
-        nc.sync.dma_start(out=lnb_bc[:], in_=ln_out_b.partition_broadcast(P))
         load_hid(6, 2)
         load_p_ln(4, 4)
+
+        def spread(dst, pick, src):
+            width = dst.shape[1]
+            spread_bank = psum_z.tile([P, BANK], F32, tag="acc")
+            nc.tensor.matmul(out=spread_bank[:, 0:width], lhsT=pick, rhs=src, start=True, stop=True)
+            nc.scalar.copy(out=dst, in_=spread_bank[:, 0:width])
+
+        def pick_row(k):
+            return ident_bf[:, k : k + 1].to_broadcast([P, P])
+
+        def spread_node_j(r):
+            spread(z_rest[:, r, 0:HD], pick_j[:, r, :], node_rows[:])
 
         def to_k_on_partitions(rows_bf16, grouped):
             words = rows_bf16.bitcast(F32)
@@ -183,7 +206,7 @@ def tile_edgeupdaterwrapper_v01_pb_kernel(
             live["s_scales", r] = s_scales
 
         def second_matmul(r):
-            acc = psum_z.tile([P, ED], F32)
+            acc = psum_z.tile([P, ED], F32, tag="acc")
             for g in range(GROUPS):
                 nc.tensor.matmul_mx(
                     out=acc[:],
@@ -241,11 +264,27 @@ def tile_edgeupdaterwrapper_v01_pb_kernel(
             if 0 <= r < TILES:
                 work_of(r)
 
-        for k in range(-3, TILES + 2):
+        spread(b2_bc[:, 0:BANK], pick_row(0), rows[:, 0:BANK])
+        spread(b2_bc[:, BANK:MD], pick_row(0), rows[:, BANK:MD])
+        turn_hid(0)
+        turn_hid(1)
+        spread(node_i[:], pick_i[:], node_rows[:])
+        spread_node_j(0)
+        spread_node_j(1)
+        quantise_hid(0)
+        quantise_hid(1)
+        first_matmul(0)
+        turn_hid(2)
+        spread(bo_bc[:], pick_row(1), rows[:, 0:ED])
+        spread(g_bc[:], pick_row(1), rows[:, ED : 2 * ED])
+        spread(lnb_bc[:], pick_row(2), rows[:, 0:ED])
+
+        for k in range(TILES + 2):
             stage(first_matmul, k + 1)
             stage(add_b2, k)
             stage(quantise_s, k - 1)
             stage(second_matmul, k - 1)
+            stage(spread_node_j, k + 2)
             stage(relu_add_z, k)
             stage(turn_s, k)
             stage(add_bo, k - 1)

@@ -67,10 +67,10 @@ def tile_edgeupdaterwrapper_v01_pb_kernel(
         hid_codes = keep.tile([P, TILES, GROUPS, P], U32, align_bytes=64)
         hid_scales = keep.tile([P, TILES, GROUPS, P], U8, align_bytes=64)
 
+        nc.vector.memset(rows[:].bitcast(I32), 0)
+        nc.vector.memset(node_rows[:].bitcast(I32), 0)
         nc.vector.memset(planes[:].bitcast(I32), 0)
         nc.vector.memset(eps[:], EPS)
-        nc.vector.memset(rows[:], 0.0)
-        nc.vector.memset(node_rows[:], 0.0)
         make_identity(nc, ident[:])
         make_identity(nc, ident_bf[:])
         nc.vector.tensor_copy(
@@ -97,9 +97,9 @@ def tile_edgeupdaterwrapper_v01_pb_kernel(
                     in_=scales[:, 4 * q : 4 * q + 4, :].bitcast(I32),
                 )
 
-        nc.sync.dma_start(out=node_rows[0:NODES, :], in_=nodes)
-        nc.sync.dma_start(out=rows[0:1, :], in_=b2.unsqueeze(0))
         load_hid(0, 2)
+        nc.sync.dma_start(out=rows[0:1, :], in_=b2.unsqueeze(0))
+        nc.sync.dma_start(out=node_rows[0:NODES, :], in_=nodes)
         load_planes(W2_scales, 0, MD)
         for h in range(MD // BANK):
             nc.sync.dma_start(
@@ -111,14 +111,14 @@ def tile_edgeupdaterwrapper_v01_pb_kernel(
         nc.sync.dma_start(out=rows[2:3, 0:ED], in_=ln_out_b.unsqueeze(0))
         load_p_ln(0, 2)
         load_hid(2, 2)
+        load_p_ln(2, 2)
         load_planes(Wo_scales, 8, ED)
         nc.sync.dma_start(
             out=wo_sb[:].bitcast(I32), in_=Wo_words.rearrange("g p n t -> p g (n t)").bitcast(I32)
         )
-        load_p_ln(2, 2)
         load_hid(4, 2)
-        load_hid(6, 2)
         load_p_ln(4, 4)
+        load_hid(6, 2)
 
         def spread(dst, pick, src):
             width = dst.shape[1]
@@ -254,20 +254,20 @@ def tile_edgeupdaterwrapper_v01_pb_kernel(
         def finish(r):
             rstd = stats.tile([P, 1], F32)
             nc.vector.reciprocal(out=rstd[:], in_=live["std", r][:])
-            normed = work.tile([P, ED], F32)
-            nc.scalar.activation(out=normed[:], in_=live["scaled", r][:], func=ACT.Copy, scale=rstd[:])
             result = work.tile([P, ED], F32)
-            nc.gpsimd.tensor_tensor(out=result[:], in0=normed[:], in1=resid[:, r, :], op=ALU.add)
+            nc.vector.scalar_tensor_tensor(
+                out=result[:], in0=live["scaled", r][:], scalar=rstd[:], in1=resid[:, r, :], op0=ALU.mult, op1=ALU.add
+            )
             nc.sync.dma_start(out=out_rows[:, r, :], in_=result[:])
 
         def stage(work_of, r):
             if 0 <= r < TILES:
                 work_of(r)
 
-        spread(b2_bc[:, 0:BANK], pick_row(0), rows[:, 0:BANK])
-        spread(b2_bc[:, BANK:MD], pick_row(0), rows[:, BANK:MD])
         turn_hid(0)
         turn_hid(1)
+        spread(b2_bc[:, 0:BANK], pick_row(0), rows[:, 0:BANK])
+        spread(b2_bc[:, BANK:MD], pick_row(0), rows[:, BANK:MD])
         spread(node_i[:], pick_i[:], node_rows[:])
         spread_node_j(0)
         spread_node_j(1)
@@ -278,6 +278,8 @@ def tile_edgeupdaterwrapper_v01_pb_kernel(
         spread(bo_bc[:], pick_row(1), rows[:, 0:ED])
         spread(g_bc[:], pick_row(1), rows[:, ED : 2 * ED])
         spread(lnb_bc[:], pick_row(2), rows[:, 0:ED])
+        for r in range(TILES):
+            residual(r)
 
         for k in range(TILES + 2):
             stage(first_matmul, k + 1)
@@ -290,7 +292,6 @@ def tile_edgeupdaterwrapper_v01_pb_kernel(
             stage(add_bo, k - 1)
             stage(quantise_hid, k + 2)
             stage(variance, k - 1)
-            stage(residual, k)
             stage(finish, k - 2)
             stage(centre_times_g, k - 1)
             stage(turn_hid, k + 3)

@@ -47,8 +47,7 @@ def tile_edgeupdaterwrapper_v01_pb_kernel(
         psum_z = ctx.enter_context(tc.psum_pool(name="psum_z", bufs=2))
 
         hid_sb = keep.tile([P, TILES, F], BF16)
-        node_i = keep.tile([P, HD], BF16)
-        z_rest = keep.tile([P, TILES, MD - HD], BF16)
+        z_in = keep.tile([P, TILES, MD], BF16)
         w2_sb = keep.tile([P, GROUPS, 4 * MD], U8, align_bytes=64)
         wo_sb = keep.tile([P, GROUPS, 4 * ED], U8, align_bytes=64)
         planes = keep.tile([P, MD], U8, align_bytes=64)
@@ -87,7 +86,7 @@ def tile_edgeupdaterwrapper_v01_pb_kernel(
 
         def load_p_ln(first, count):
             nc.sync.dma_start(
-                out=z_rest[:, first : first + count, HD : MD - HD], in_=p_ln_rows[:, first : first + count, :]
+                out=z_in[:, first : first + count, 2 * HD : MD], in_=p_ln_rows[:, first : first + count, :]
             )
 
         def load_planes(scales, first_row, width):
@@ -129,8 +128,17 @@ def tile_edgeupdaterwrapper_v01_pb_kernel(
         def pick_row(k):
             return ident_bf[:, k : k + 1].to_broadcast([P, P])
 
-        def spread_node_j(r):
-            spread(z_rest[:, r, 0:HD], pick_j[:, r, :], node_rows[:])
+        def spread_nodes(r):
+            node_bank = psum_z.tile([P, BANK], F32, tag="acc")
+            nc.tensor.matmul(out=node_bank[:, 0:HD], lhsT=pick_i[:], rhs=node_rows[:], start=True, stop=True)
+            nc.tensor.matmul(out=node_bank[:, HD : 2 * HD], lhsT=pick_j[:, r, :], rhs=node_rows[:], start=True, stop=True)
+            nc.scalar.copy(out=z_in[:, r, 0 : 2 * HD], in_=node_bank[:])
+
+        ln_rows = [(bo_bc, 1, 0), (g_bc, 1, ED), (lnb_bc, 2, 0)]
+
+        def spread_ln_row(n):
+            dst, k, first = ln_rows[n]
+            spread(dst[:], pick_row(k), rows[:, first : first + ED])
 
         def to_k_on_partitions(rows_bf16, grouped):
             words = rows_bf16.bitcast(F32)
@@ -186,10 +194,7 @@ def tile_edgeupdaterwrapper_v01_pb_kernel(
             pre = live["pre", r]
             s_sb = work.tile([P, MD], BF16)
             nc.vector.scalar_tensor_tensor(
-                out=s_sb[:, 0:HD], in0=pre[:, 0:HD], scalar=0.0, in1=node_i[:], op0=ALU.max, op1=ALU.add
-            )
-            nc.vector.scalar_tensor_tensor(
-                out=s_sb[:, HD:MD], in0=pre[:, HD:MD], scalar=0.0, in1=z_rest[:, r, :], op0=ALU.max, op1=ALU.add
+                out=s_sb[:], in0=pre[:], scalar=0.0, in1=z_in[:, r, :], op0=ALU.max, op1=ALU.add
             )
             live["s", r] = s_sb
 
@@ -230,16 +235,16 @@ def tile_edgeupdaterwrapper_v01_pb_kernel(
 
         def variance(r):
             neg_mean = stats.tile([P, 1], F32)
-            nc.vector.tensor_scalar_mul(out=neg_mean[:], in0=live["z_sum", r][:], scalar1=-1.0 / ED)
+            nc.scalar.mul(out=neg_mean[:], in_=live["z_sum", r][:], mul=-1.0 / ED)
             squares = work.tile([P, ED], F32)
             sq_sum = stats.tile([P, 1], F32)
             nc.scalar.activation(
                 out=squares[:], in_=live["z", r][:], func=ACT.Square, bias=neg_mean[:], scale=1.0, accum_out=sq_sum[:]
             )
-            std = stats.tile([P, 1], F32)
-            nc.scalar.activation(out=std[:], in_=sq_sum[:], func=ACT.Sqrt, bias=eps[:], scale=1.0 / ED)
+            rstd = stats.tile([P, 1], F32)
+            nc.scalar.activation(out=rstd[:], in_=sq_sum[:], func=ACT.Abs_reciprocal_sqrt, bias=eps[:], scale=1.0 / ED)
             live["neg_mean", r] = neg_mean
-            live["std", r] = std
+            live["rstd", r] = rstd
 
         def centre_times_g(r):
             scaled = work.tile([P, ED], F32)
@@ -249,14 +254,12 @@ def tile_edgeupdaterwrapper_v01_pb_kernel(
             live["scaled", r] = scaled
 
         def residual(r):
-            nc.gpsimd.tensor_tensor(out=resid[:, r, :], in0=z_rest[:, r, HD : MD - HD], in1=lnb_bc[:], op=ALU.add)
+            nc.gpsimd.tensor_tensor(out=resid[:, r, :], in0=z_in[:, r, 2 * HD : MD], in1=lnb_bc[:], op=ALU.add)
 
         def finish(r):
-            rstd = stats.tile([P, 1], F32)
-            nc.vector.reciprocal(out=rstd[:], in_=live["std", r][:])
             result = work.tile([P, ED], F32)
             nc.vector.scalar_tensor_tensor(
-                out=result[:], in0=live["scaled", r][:], scalar=rstd[:], in1=resid[:, r, :], op0=ALU.mult, op1=ALU.add
+                out=result[:], in0=live["scaled", r][:], scalar=live["rstd", r][:], in1=resid[:, r, :], op0=ALU.mult, op1=ALU.add
             )
             nc.sync.dma_start(out=out_rows[:, r, :], in_=result[:])
 
@@ -265,33 +268,30 @@ def tile_edgeupdaterwrapper_v01_pb_kernel(
                 work_of(r)
 
         turn_hid(0)
-        turn_hid(1)
         spread(b2_bc[:, 0:BANK], pick_row(0), rows[:, 0:BANK])
         spread(b2_bc[:, BANK:MD], pick_row(0), rows[:, BANK:MD])
-        spread(node_i[:], pick_i[:], node_rows[:])
-        spread_node_j(0)
-        spread_node_j(1)
+        turn_hid(1)
         quantise_hid(0)
-        quantise_hid(1)
         first_matmul(0)
+        spread_nodes(0)
+        quantise_hid(1)
+        spread_nodes(1)
         turn_hid(2)
-        spread(bo_bc[:], pick_row(1), rows[:, 0:ED])
-        spread(g_bc[:], pick_row(1), rows[:, ED : 2 * ED])
-        spread(lnb_bc[:], pick_row(2), rows[:, 0:ED])
-        for r in range(TILES):
-            residual(r)
 
-        for k in range(TILES + 2):
+        for k in range(TILES + 3):
+            stage(turn_s, k - 1)
+            stage(second_matmul, k - 2)
             stage(first_matmul, k + 1)
-            stage(add_b2, k)
-            stage(quantise_s, k - 1)
-            stage(second_matmul, k - 1)
-            stage(spread_node_j, k + 2)
-            stage(relu_add_z, k)
-            stage(turn_s, k)
-            stage(add_bo, k - 1)
-            stage(quantise_hid, k + 2)
-            stage(variance, k - 1)
-            stage(finish, k - 2)
-            stage(centre_times_g, k - 1)
+            stage(spread_nodes, k + 2)
             stage(turn_hid, k + 3)
+            if k < len(ln_rows):
+                spread_ln_row(k)
+            stage(add_b2, k)
+            stage(relu_add_z, k)
+            stage(quantise_s, k - 1)
+            stage(add_bo, k - 2)
+            stage(quantise_hid, k + 2)
+            stage(variance, k - 2)
+            stage(residual, k - 2)
+            stage(finish, k - 3)
+            stage(centre_times_g, k - 2)

@@ -71,7 +71,7 @@ def tile_edgeupdaterwrapper_v01_pb_kernel(
         nc.vector.memset(planes[:].bitcast(I32), 0)
         nc.vector.memset(eps[:], EPS)
         make_identity(nc, ident[:])
-        make_identity(nc, ident_bf[:])
+        nc.vector.tensor_copy(out=ident_bf[:], in_=ident[:])
         nc.vector.tensor_copy(
             out=pick_i[:].rearrange("k (q a) -> k q a", a=4),
             in_=ident_bf[:, 0:NODES].unsqueeze(2).to_broadcast([P, NODES, 4]),
@@ -89,17 +89,17 @@ def tile_edgeupdaterwrapper_v01_pb_kernel(
                 out=z_in[:, first : first + count, 2 * HD : MD], in_=p_ln_rows[:, first : first + count, :]
             )
 
-        def load_planes(scales, first_row, width):
+        def load_planes(queue, view, scales, first_row, width):
             for q in range(4):
-                nc.sync.dma_start(
-                    out=planes[32 * q + first_row : 32 * q + first_row + 8, 0:width].bitcast(I32),
-                    in_=scales[:, 4 * q : 4 * q + 4, :].bitcast(I32),
+                queue.dma_start(
+                    out=planes[32 * q + first_row : 32 * q + first_row + 8, 0:width].bitcast(view),
+                    in_=scales[:, 4 * q : 4 * q + 4, :].bitcast(view),
                 )
 
         load_hid(0, 2)
-        nc.sync.dma_start(out=rows[0:1, :], in_=b2.unsqueeze(0))
-        nc.sync.dma_start(out=node_rows[0:NODES, :], in_=nodes)
-        load_planes(W2_scales, 0, MD)
+        load_planes(nc.scalar, F32, W2_scales, 0, MD)
+        nc.scalar.dma_start(out=rows[0:1, :], in_=b2.unsqueeze(0))
+        nc.scalar.dma_start(out=node_rows[0:NODES, :], in_=nodes)
         for h in range(MD // BANK):
             nc.sync.dma_start(
                 out=w2_sb[:, :, 4 * BANK * h : 4 * BANK * (h + 1)].bitcast(I32),
@@ -111,7 +111,7 @@ def tile_edgeupdaterwrapper_v01_pb_kernel(
         load_p_ln(0, 2)
         load_hid(2, 2)
         load_p_ln(2, 2)
-        load_planes(Wo_scales, 8, ED)
+        load_planes(nc.sync, I32, Wo_scales, 8, ED)
         nc.sync.dma_start(
             out=wo_sb[:].bitcast(I32), in_=Wo_words.rearrange("g p n t -> p g (n t)").bitcast(I32)
         )
@@ -257,10 +257,10 @@ def tile_edgeupdaterwrapper_v01_pb_kernel(
             nc.gpsimd.tensor_tensor(out=resid[:, r, :], in0=z_in[:, r, 2 * HD : MD], in1=lnb_bc[:], op=ALU.add)
 
         def finish(r):
+            normed = work.tile([P, ED], F32)
+            nc.scalar.activation(out=normed[:], in_=live["scaled", r][:], func=ACT.Copy, scale=live["rstd", r][:])
             result = work.tile([P, ED], F32)
-            nc.vector.scalar_tensor_tensor(
-                out=result[:], in0=live["scaled", r][:], scalar=live["rstd", r][:], in1=resid[:, r, :], op0=ALU.mult, op1=ALU.add
-            )
+            nc.gpsimd.tensor_tensor(out=result[:], in0=normed[:], in1=resid[:, r, :], op=ALU.add)
             nc.sync.dma_start(out=out_rows[:, r, :], in_=result[:])
 
         def stage(work_of, r):
@@ -279,6 +279,7 @@ def tile_edgeupdaterwrapper_v01_pb_kernel(
         turn_hid(2)
 
         for k in range(TILES + 3):
+            stage(finish, k - 3)
             stage(turn_s, k - 1)
             stage(second_matmul, k - 2)
             stage(first_matmul, k + 1)
@@ -293,5 +294,4 @@ def tile_edgeupdaterwrapper_v01_pb_kernel(
             stage(quantise_hid, k + 2)
             stage(variance, k - 2)
             stage(residual, k - 2)
-            stage(finish, k - 3)
             stage(centre_times_g, k - 2)

@@ -23,6 +23,7 @@ MD = 1024
 GROUPS = 2
 BANK = 512
 EPS = 1e-5
+GPSIMD_TILES = TILES // 2
 
 FLOPS = 2 * EDGES * F * MD + 2 * EDGES * MD * ED
 
@@ -41,7 +42,7 @@ def tile_edgeupdaterwrapper_v01_pb_kernel(
         ctx.enter_context(tc.manual_schedule())
         keep = ctx.enter_context(tc.tile_pool(name="keep", bufs=1))
         work = ctx.enter_context(tc.tile_pool(name="work", bufs=3))
-        stats = ctx.enter_context(tc.tile_pool(name="stats", bufs=4))
+        stats = ctx.enter_context(tc.tile_pool(name="stats", bufs=TILES))
         psum_t = ctx.enter_context(tc.psum_pool(name="psum_t", bufs=2))
         psum_y = ctx.enter_context(tc.psum_pool(name="psum_y", bufs=4))
         psum_z = ctx.enter_context(tc.psum_pool(name="psum_z", bufs=2))
@@ -61,6 +62,7 @@ def tile_edgeupdaterwrapper_v01_pb_kernel(
         g_bc = keep.tile([P, ED], BF16)
         lnb_bc = keep.tile([P, ED], BF16)
         resid = keep.tile([P, TILES, ED], F32)
+        z_all = keep.tile([P, TILES, ED], F32)
         ident = keep.tile([P, P], F32)
         eps = keep.tile([P, 1], F32)
         hid_codes = keep.tile([P, TILES, GROUPS, P], U32, align_bytes=64)
@@ -71,7 +73,7 @@ def tile_edgeupdaterwrapper_v01_pb_kernel(
         nc.vector.memset(planes[:].bitcast(I32), 0)
         nc.vector.memset(eps[:], EPS)
         make_identity(nc, ident[:])
-        nc.vector.tensor_copy(out=ident_bf[:], in_=ident[:])
+        make_identity(nc, ident_bf[:])
         nc.vector.tensor_copy(
             out=pick_i[:].rearrange("k (q a) -> k q a", a=4),
             in_=ident_bf[:, 0:NODES].unsqueeze(2).to_broadcast([P, NODES, 4]),
@@ -89,17 +91,17 @@ def tile_edgeupdaterwrapper_v01_pb_kernel(
                 out=z_in[:, first : first + count, 2 * HD : MD], in_=p_ln_rows[:, first : first + count, :]
             )
 
-        def load_planes(queue, view, scales, first_row, width):
+        def load_planes(scales, first_row, width):
             for q in range(4):
-                queue.dma_start(
-                    out=planes[32 * q + first_row : 32 * q + first_row + 8, 0:width].bitcast(view),
-                    in_=scales[:, 4 * q : 4 * q + 4, :].bitcast(view),
+                nc.sync.dma_start(
+                    out=planes[32 * q + first_row : 32 * q + first_row + 8, 0:width].bitcast(I32),
+                    in_=scales[:, 4 * q : 4 * q + 4, :].bitcast(I32),
                 )
 
         load_hid(0, 2)
-        load_planes(nc.scalar, F32, W2_scales, 0, MD)
-        nc.scalar.dma_start(out=rows[0:1, :], in_=b2.unsqueeze(0))
-        nc.scalar.dma_start(out=node_rows[0:NODES, :], in_=nodes)
+        nc.sync.dma_start(out=rows[0:1, :], in_=b2.unsqueeze(0))
+        nc.sync.dma_start(out=node_rows[0:NODES, :], in_=nodes)
+        load_planes(W2_scales, 0, MD)
         for h in range(MD // BANK):
             nc.sync.dma_start(
                 out=w2_sb[:, :, 4 * BANK * h : 4 * BANK * (h + 1)].bitcast(I32),
@@ -111,7 +113,7 @@ def tile_edgeupdaterwrapper_v01_pb_kernel(
         load_p_ln(0, 2)
         load_hid(2, 2)
         load_p_ln(2, 2)
-        load_planes(nc.sync, I32, Wo_scales, 8, ED)
+        load_planes(Wo_scales, 8, ED)
         nc.sync.dma_start(
             out=wo_sb[:].bitcast(I32), in_=Wo_words.rearrange("g p n t -> p g (n t)").bitcast(I32)
         )
@@ -134,7 +136,7 @@ def tile_edgeupdaterwrapper_v01_pb_kernel(
             nc.tensor.matmul(out=node_bank[:, HD : 2 * HD], lhsT=pick_j[:, r, :], rhs=node_rows[:], start=True, stop=True)
             nc.scalar.copy(out=z_in[:, r, 0 : 2 * HD], in_=node_bank[:])
 
-        ln_rows = [(bo_bc, 1, 0), (g_bc, 1, ED), (lnb_bc, 2, 0)]
+        ln_rows = [(lnb_bc, 2, 0), (bo_bc, 1, 0), (g_bc, 1, ED)]
 
         def spread_ln_row(n):
             dst, k, first = ln_rows[n]
@@ -225,21 +227,20 @@ def tile_edgeupdaterwrapper_v01_pb_kernel(
             live["acc", r] = acc
 
         def add_bo(r):
-            z = work.tile([P, ED], F32)
             z_sum = stats.tile([P, 1], F32)
             nc.vector.scalar_tensor_tensor(
-                out=z[:], in0=live["acc", r][:], scalar=1.0, in1=bo_bc[:], op0=ALU.mult, op1=ALU.add, accum_out=z_sum[:]
+                out=z_all[:, r, :], in0=live["acc", r][:], scalar=1.0, in1=bo_bc[:], op0=ALU.mult, op1=ALU.add,
+                accum_out=z_sum[:],
             )
-            live["z", r] = z
             live["z_sum", r] = z_sum
 
         def variance(r):
             neg_mean = stats.tile([P, 1], F32)
-            nc.scalar.mul(out=neg_mean[:], in_=live["z_sum", r][:], mul=-1.0 / ED)
+            nc.vector.tensor_scalar_mul(out=neg_mean[:], in0=live["z_sum", r][:], scalar1=-1.0 / ED)
             squares = work.tile([P, ED], F32)
             sq_sum = stats.tile([P, 1], F32)
             nc.scalar.activation(
-                out=squares[:], in_=live["z", r][:], func=ACT.Square, bias=neg_mean[:], scale=1.0, accum_out=sq_sum[:]
+                out=squares[:], in_=z_all[:, r, :], func=ACT.Square, bias=neg_mean[:], scale=1.0, accum_out=sq_sum[:]
             )
             rstd = stats.tile([P, 1], F32)
             nc.scalar.activation(out=rstd[:], in_=sq_sum[:], func=ACT.Abs_reciprocal_sqrt, bias=eps[:], scale=1.0 / ED)
@@ -247,20 +248,32 @@ def tile_edgeupdaterwrapper_v01_pb_kernel(
             live["rstd", r] = rstd
 
         def centre_times_g(r):
-            scaled = work.tile([P, ED], F32)
-            nc.vector.scalar_tensor_tensor(
-                out=scaled[:], in0=live["z", r][:], scalar=live["neg_mean", r][:], in1=g_bc[:], op0=ALU.add, op1=ALU.mult
-            )
-            live["scaled", r] = scaled
+            if r >= GPSIMD_TILES:
+                scaled = work.tile([P, ED], F32)
+                nc.vector.scalar_tensor_tensor(
+                    out=scaled[:], in0=z_all[:, r, :], scalar=live["neg_mean", r][:], in1=g_bc[:], op0=ALU.add, op1=ALU.mult
+                )
+                live["scaled", r] = scaled
 
         def residual(r):
             nc.gpsimd.tensor_tensor(out=resid[:, r, :], in0=z_in[:, r, 2 * HD : MD], in1=lnb_bc[:], op=ALU.add)
 
         def finish(r):
-            normed = work.tile([P, ED], F32)
-            nc.scalar.activation(out=normed[:], in_=live["scaled", r][:], func=ACT.Copy, scale=live["rstd", r][:])
             result = work.tile([P, ED], F32)
-            nc.gpsimd.tensor_tensor(out=result[:], in0=normed[:], in1=resid[:, r, :], op=ALU.add)
+            if r < GPSIMD_TILES:
+                normed = work.tile([P, ED], F32)
+                nc.gpsimd.tensor_scalar(
+                    out=normed[:], in0=z_all[:, r, :], scalar1=live["neg_mean", r][:], scalar2=live["rstd", r][:],
+                    op0=ALU.add, op1=ALU.mult,
+                )
+                scaled = work.tile([P, ED], F32)
+                nc.gpsimd.tensor_tensor(out=scaled[:], in0=normed[:], in1=g_bc[:], op=ALU.mult)
+                nc.gpsimd.tensor_tensor(out=result[:], in0=scaled[:], in1=resid[:, r, :], op=ALU.add)
+            else:
+                nc.vector.scalar_tensor_tensor(
+                    out=result[:], in0=live["scaled", r][:], scalar=live["rstd", r][:], in1=resid[:, r, :],
+                    op0=ALU.mult, op1=ALU.add,
+                )
             nc.sync.dma_start(out=out_rows[:, r, :], in_=result[:])
 
         def stage(work_of, r):
@@ -279,7 +292,6 @@ def tile_edgeupdaterwrapper_v01_pb_kernel(
         turn_hid(2)
 
         for k in range(TILES + 3):
-            stage(finish, k - 3)
             stage(turn_s, k - 1)
             stage(second_matmul, k - 2)
             stage(first_matmul, k + 1)
@@ -287,11 +299,14 @@ def tile_edgeupdaterwrapper_v01_pb_kernel(
             stage(turn_hid, k + 3)
             if k < len(ln_rows):
                 spread_ln_row(k)
+            if k == 0:
+                for r in range(TILES):
+                    residual(r)
             stage(add_b2, k)
             stage(relu_add_z, k)
-            stage(quantise_s, k - 1)
             stage(add_bo, k - 2)
-            stage(quantise_hid, k + 2)
+            stage(quantise_s, k - 1)
             stage(variance, k - 2)
-            stage(residual, k - 2)
+            stage(quantise_hid, k + 2)
+            stage(finish, k - 3)
             stage(centre_times_g, k - 2)

@@ -68,10 +68,10 @@ def tile_edgeupdaterwrapper_v01_pb_kernel(
         hid_codes = keep.tile([P, TILES, GROUPS, P], U32, align_bytes=64)
         hid_scales = keep.tile([P, TILES, GROUPS, P], U8, align_bytes=64)
 
+        nc.vector.memset(eps[:], EPS)
+        nc.vector.memset(planes[:].bitcast(I32), 0)
         nc.vector.memset(rows[:].bitcast(I32), 0)
         nc.vector.memset(node_rows[:].bitcast(I32), 0)
-        nc.vector.memset(planes[:].bitcast(I32), 0)
-        nc.vector.memset(eps[:], EPS)
         make_identity(nc, ident[:])
         make_identity(nc, ident_bf[:])
         nc.vector.tensor_copy(
@@ -91,29 +91,31 @@ def tile_edgeupdaterwrapper_v01_pb_kernel(
                 out=z_in[:, first : first + count, 2 * HD : MD], in_=p_ln_rows[:, first : first + count, :]
             )
 
-        def load_planes(scales, first_row, width):
+        def load_planes(queue, word, scales, first_row, width):
             for q in range(4):
-                nc.sync.dma_start(
-                    out=planes[32 * q + first_row : 32 * q + first_row + 8, 0:width].bitcast(I32),
-                    in_=scales[:, 4 * q : 4 * q + 4, :].bitcast(I32),
+                queue.dma_start(
+                    out=planes[32 * q + first_row : 32 * q + first_row + 8, 0:width].bitcast(word),
+                    in_=scales[:, 4 * q : 4 * q + 4, :].bitcast(word),
                 )
 
+        table_warm = keep.tile([P, 1], F32)
+        nc.scalar.activation(out=table_warm[:], in_=eps[:], func=ACT.Abs_reciprocal_sqrt)
         load_hid(0, 2)
-        nc.sync.dma_start(out=rows[0:1, :], in_=b2.unsqueeze(0))
-        nc.sync.dma_start(out=node_rows[0:NODES, :], in_=nodes)
-        load_planes(W2_scales, 0, MD)
+        load_planes(nc.scalar, F32, W2_scales, 0, MD)
+        nc.scalar.dma_start(out=rows[0:1, :], in_=b2.unsqueeze(0))
+        nc.scalar.dma_start(out=node_rows[0:NODES, :], in_=nodes)
         for h in range(MD // BANK):
             nc.sync.dma_start(
                 out=w2_sb[:, :, 4 * BANK * h : 4 * BANK * (h + 1)].bitcast(I32),
                 in_=W2_words[:, :, BANK * h : BANK * (h + 1), :].rearrange("g p n t -> p g (n t)").bitcast(I32),
             )
+        nc.sync.dma_start(out=rows[2:3, 0:ED], in_=ln_out_b.unsqueeze(0))
         nc.sync.dma_start(out=rows[1:2, 0:ED], in_=bo.unsqueeze(0))
         nc.sync.dma_start(out=rows[1:2, ED : 2 * ED], in_=ln_out_g.unsqueeze(0))
-        nc.sync.dma_start(out=rows[2:3, 0:ED], in_=ln_out_b.unsqueeze(0))
         load_p_ln(0, 2)
         load_hid(2, 2)
         load_p_ln(2, 2)
-        load_planes(Wo_scales, 8, ED)
+        load_planes(nc.sync, I32, Wo_scales, 8, ED)
         nc.sync.dma_start(
             out=wo_sb[:].bitcast(I32), in_=Wo_words.rearrange("g p n t -> p g (n t)").bitcast(I32)
         )

@@ -23,7 +23,6 @@ MD = 1024
 GROUPS = 2
 BANK = 512
 EPS = 1e-5
-GPSIMD_TILES = TILES // 2
 
 FLOPS = 2 * EDGES * F * MD + 2 * EDGES * MD * ED
 
@@ -42,7 +41,7 @@ def tile_edgeupdaterwrapper_v01_pb_kernel(
         ctx.enter_context(tc.manual_schedule())
         keep = ctx.enter_context(tc.tile_pool(name="keep", bufs=1))
         work = ctx.enter_context(tc.tile_pool(name="work", bufs=3))
-        stats = ctx.enter_context(tc.tile_pool(name="stats", bufs=TILES))
+        stats = ctx.enter_context(tc.tile_pool(name="stats", bufs=4))
         psum_t = ctx.enter_context(tc.psum_pool(name="psum_t", bufs=2))
         psum_y = ctx.enter_context(tc.psum_pool(name="psum_y", bufs=4))
         psum_z = ctx.enter_context(tc.psum_pool(name="psum_z", bufs=2))
@@ -62,16 +61,15 @@ def tile_edgeupdaterwrapper_v01_pb_kernel(
         g_bc = keep.tile([P, ED], BF16)
         lnb_bc = keep.tile([P, ED], BF16)
         resid = keep.tile([P, TILES, ED], F32)
-        z_all = keep.tile([P, TILES, ED], F32)
         ident = keep.tile([P, P], F32)
         eps = keep.tile([P, 1], F32)
         hid_codes = keep.tile([P, TILES, GROUPS, P], U32, align_bytes=64)
         hid_scales = keep.tile([P, TILES, GROUPS, P], U8, align_bytes=64)
 
         nc.vector.memset(eps[:], EPS)
-        nc.vector.memset(planes[:].bitcast(I32), 0)
         nc.vector.memset(rows[:].bitcast(I32), 0)
         nc.vector.memset(node_rows[:].bitcast(I32), 0)
+        nc.vector.memset(planes[:].bitcast(I32), 0)
         make_identity(nc, ident[:])
         make_identity(nc, ident_bf[:])
         nc.vector.tensor_copy(
@@ -91,31 +89,32 @@ def tile_edgeupdaterwrapper_v01_pb_kernel(
                 out=z_in[:, first : first + count, 2 * HD : MD], in_=p_ln_rows[:, first : first + count, :]
             )
 
-        def load_planes(queue, word, scales, first_row, width):
+        def load_planes(scales, first_row, width):
             for q in range(4):
-                queue.dma_start(
-                    out=planes[32 * q + first_row : 32 * q + first_row + 8, 0:width].bitcast(word),
-                    in_=scales[:, 4 * q : 4 * q + 4, :].bitcast(word),
+                nc.sync.dma_start(
+                    out=planes[32 * q + first_row : 32 * q + first_row + 8, 0:width].bitcast(I32),
+                    in_=scales[:, 4 * q : 4 * q + 4, :].bitcast(I32),
                 )
 
         table_warm = keep.tile([P, 1], F32)
         nc.scalar.activation(out=table_warm[:], in_=eps[:], func=ACT.Abs_reciprocal_sqrt)
+
         load_hid(0, 2)
-        load_planes(nc.scalar, F32, W2_scales, 0, MD)
-        nc.scalar.dma_start(out=rows[0:1, :], in_=b2.unsqueeze(0))
-        nc.scalar.dma_start(out=node_rows[0:NODES, :], in_=nodes)
+        nc.sync.dma_start(out=rows[0:1, :], in_=b2.unsqueeze(0))
+        nc.sync.dma_start(out=node_rows[0:NODES, :], in_=nodes)
+        load_planes(W2_scales, 0, MD)
         for h in range(MD // BANK):
             nc.sync.dma_start(
                 out=w2_sb[:, :, 4 * BANK * h : 4 * BANK * (h + 1)].bitcast(I32),
                 in_=W2_words[:, :, BANK * h : BANK * (h + 1), :].rearrange("g p n t -> p g (n t)").bitcast(I32),
             )
-        nc.sync.dma_start(out=rows[2:3, 0:ED], in_=ln_out_b.unsqueeze(0))
         nc.sync.dma_start(out=rows[1:2, 0:ED], in_=bo.unsqueeze(0))
         nc.sync.dma_start(out=rows[1:2, ED : 2 * ED], in_=ln_out_g.unsqueeze(0))
+        nc.sync.dma_start(out=rows[2:3, 0:ED], in_=ln_out_b.unsqueeze(0))
         load_p_ln(0, 2)
         load_hid(2, 2)
         load_p_ln(2, 2)
-        load_planes(nc.sync, I32, Wo_scales, 8, ED)
+        load_planes(Wo_scales, 8, ED)
         nc.sync.dma_start(
             out=wo_sb[:].bitcast(I32), in_=Wo_words.rearrange("g p n t -> p g (n t)").bitcast(I32)
         )
@@ -229,11 +228,12 @@ def tile_edgeupdaterwrapper_v01_pb_kernel(
             live["acc", r] = acc
 
         def add_bo(r):
+            z = work.tile([P, ED], F32)
             z_sum = stats.tile([P, 1], F32)
             nc.vector.scalar_tensor_tensor(
-                out=z_all[:, r, :], in0=live["acc", r][:], scalar=1.0, in1=bo_bc[:], op0=ALU.mult, op1=ALU.add,
-                accum_out=z_sum[:],
+                out=z[:], in0=live["acc", r][:], scalar=1.0, in1=bo_bc[:], op0=ALU.mult, op1=ALU.add, accum_out=z_sum[:]
             )
+            live["z", r] = z
             live["z_sum", r] = z_sum
 
         def variance(r):
@@ -242,7 +242,7 @@ def tile_edgeupdaterwrapper_v01_pb_kernel(
             squares = work.tile([P, ED], F32)
             sq_sum = stats.tile([P, 1], F32)
             nc.scalar.activation(
-                out=squares[:], in_=z_all[:, r, :], func=ACT.Square, bias=neg_mean[:], scale=1.0, accum_out=sq_sum[:]
+                out=squares[:], in_=live["z", r][:], func=ACT.Square, bias=neg_mean[:], scale=1.0, accum_out=sq_sum[:]
             )
             rstd = stats.tile([P, 1], F32)
             nc.scalar.activation(out=rstd[:], in_=sq_sum[:], func=ACT.Abs_reciprocal_sqrt, bias=eps[:], scale=1.0 / ED)
@@ -250,32 +250,20 @@ def tile_edgeupdaterwrapper_v01_pb_kernel(
             live["rstd", r] = rstd
 
         def centre_times_g(r):
-            if r >= GPSIMD_TILES:
-                scaled = work.tile([P, ED], F32)
-                nc.vector.scalar_tensor_tensor(
-                    out=scaled[:], in0=z_all[:, r, :], scalar=live["neg_mean", r][:], in1=g_bc[:], op0=ALU.add, op1=ALU.mult
-                )
-                live["scaled", r] = scaled
+            scaled = work.tile([P, ED], F32)
+            nc.vector.scalar_tensor_tensor(
+                out=scaled[:], in0=live["z", r][:], scalar=live["neg_mean", r][:], in1=g_bc[:], op0=ALU.add, op1=ALU.mult
+            )
+            live["scaled", r] = scaled
 
         def residual(r):
             nc.gpsimd.tensor_tensor(out=resid[:, r, :], in0=z_in[:, r, 2 * HD : MD], in1=lnb_bc[:], op=ALU.add)
 
         def finish(r):
             result = work.tile([P, ED], F32)
-            if r < GPSIMD_TILES:
-                normed = work.tile([P, ED], F32)
-                nc.gpsimd.tensor_scalar(
-                    out=normed[:], in0=z_all[:, r, :], scalar1=live["neg_mean", r][:], scalar2=live["rstd", r][:],
-                    op0=ALU.add, op1=ALU.mult,
-                )
-                scaled = work.tile([P, ED], F32)
-                nc.gpsimd.tensor_tensor(out=scaled[:], in0=normed[:], in1=g_bc[:], op=ALU.mult)
-                nc.gpsimd.tensor_tensor(out=result[:], in0=scaled[:], in1=resid[:, r, :], op=ALU.add)
-            else:
-                nc.vector.scalar_tensor_tensor(
-                    out=result[:], in0=live["scaled", r][:], scalar=live["rstd", r][:], in1=resid[:, r, :],
-                    op0=ALU.mult, op1=ALU.add,
-                )
+            nc.vector.scalar_tensor_tensor(
+                out=result[:], in0=live["scaled", r][:], scalar=live["rstd", r][:], in1=resid[:, r, :], op0=ALU.mult, op1=ALU.add
+            )
             nc.sync.dma_start(out=out_rows[:, r, :], in_=result[:])
 
         def stage(work_of, r):

@@ -21,7 +21,7 @@ ED = 512
 F = 1024
 MD = 1024
 GROUPS = 2
-BANK = 512
+PACK = 4
 EPS = 1e-5
 
 FLOPS = 2 * EDGES * F * MD + 2 * EDGES * MD * ED
@@ -42,21 +42,25 @@ def tile_edgeupdaterwrapper_v01_pb_kernel(
         keep = ctx.enter_context(tc.tile_pool(name="keep", bufs=1))
         work = ctx.enter_context(tc.tile_pool(name="work", bufs=3))
         stats = ctx.enter_context(tc.tile_pool(name="stats", bufs=4))
-        psum_t = ctx.enter_context(tc.psum_pool(name="psum_t", bufs=2))
+        psum_t = ctx.enter_context(tc.psum_pool(name="psum_t", bufs=1))
+        psum_p = ctx.enter_context(tc.psum_pool(name="psum_p", bufs=1))
         psum_y = ctx.enter_context(tc.psum_pool(name="psum_y", bufs=4))
         psum_z = ctx.enter_context(tc.psum_pool(name="psum_z", bufs=2))
 
         hid_sb = keep.tile([P, TILES, F], BF16)
-        z_in = keep.tile([P, TILES, MD], BF16)
-        w2_sb = keep.tile([P, GROUPS, 4 * MD], U8, align_bytes=64)
+        p_ln_sb = keep.tile([P, TILES, ED], BF16)
+        w2_raw = keep.tile([P, GROUPS, MD], I32, align_bytes=64)
+        w2_raw_scales = keep.tile([P, MD], U8, align_bytes=64)
+        w2_sb = keep.tile([P, GROUPS, MD], I32, align_bytes=64)
+        w2_scales = keep.tile([P, MD], U8, align_bytes=64)
         wo_sb = keep.tile([P, GROUPS, 4 * ED], U8, align_bytes=64)
-        planes = keep.tile([P, MD], U8, align_bytes=64)
-        rows = keep.tile([P, MD], BF16)
-        node_rows = keep.tile([P, HD], BF16)
+        wo_scales = keep.tile([P, ED], U8, align_bytes=64)
+        rows = keep.tile([P, 2 * ED], BF16)
+        node_rows = keep.tile([P, 2 * HD], BF16)
+        b2_cols = keep.tile([P, GROUPS, PACK], BF16)
+        x_turned = keep.tile([P, NODES, PACK], BF16)
+        z_nodes = keep.tile([P, 3, P, PACK], BF16)
         ident_bf = keep.tile([P, P], BF16)
-        pick_i = keep.tile([P, P], BF16)
-        pick_j = keep.tile([P, TILES, P], BF16)
-        b2_bc = keep.tile([P, MD], BF16)
         bo_bc = keep.tile([P, ED], BF16)
         g_bc = keep.tile([P, ED], BF16)
         lnb_bc = keep.tile([P, ED], BF16)
@@ -67,149 +71,178 @@ def tile_edgeupdaterwrapper_v01_pb_kernel(
         hid_scales = keep.tile([P, TILES, GROUPS, P], U8, align_bytes=64)
 
         nc.vector.memset(eps[:], EPS)
-        nc.vector.memset(rows[:].bitcast(I32), 0)
         nc.vector.memset(node_rows[:].bitcast(I32), 0)
-        nc.vector.memset(planes[:].bitcast(I32), 0)
+        nc.vector.memset(w2_raw_scales[:].bitcast(I32), 0)
+        nc.vector.memset(wo_scales[:].bitcast(I32), 0)
+        nc.vector.memset(rows[:].bitcast(I32), 0)
         make_identity(nc, ident[:])
         make_identity(nc, ident_bf[:])
-        nc.vector.tensor_copy(
-            out=pick_i[:].rearrange("k (q a) -> k q a", a=4),
-            in_=ident_bf[:, 0:NODES].unsqueeze(2).to_broadcast([P, NODES, 4]),
-        )
-        nc.vector.tensor_copy(
-            out=pick_j[:].rearrange("k r (q a) -> k r q a", a=4),
-            in_=ident_bf[:, 0:NODES].rearrange("k (a r) -> k r a", r=TILES).unsqueeze(2).to_broadcast([P, TILES, NODES, 4]),
-        )
 
         def load_hid(first, count):
             nc.sync.dma_start(out=hid_sb[:, first : first + count, :], in_=hid_rows[:, first : first + count, :])
 
         def load_p_ln(first, count):
-            nc.sync.dma_start(
-                out=z_in[:, first : first + count, 2 * HD : MD], in_=p_ln_rows[:, first : first + count, :]
-            )
+            nc.sync.dma_start(out=p_ln_sb[:, first : first + count, :], in_=p_ln_rows[:, first : first + count, :])
 
-        def load_planes(scales, first_row, width):
+        def load_planes(dst, scales):
             for q in range(4):
                 nc.sync.dma_start(
-                    out=planes[32 * q + first_row : 32 * q + first_row + 8, 0:width].bitcast(I32),
+                    out=dst[32 * q : 32 * q + 8, :].bitcast(I32),
                     in_=scales[:, 4 * q : 4 * q + 4, :].bitcast(I32),
                 )
+
+        def load_w2(h):
+            nc.sync.dma_start(
+                out=w2_raw[:, :, 512 * h : 512 * (h + 1)],
+                in_=W2_words[:, :, 512 * h : 512 * (h + 1), :].rearrange("g p n t -> p g (n t)").bitcast(I32),
+            )
 
         table_warm = keep.tile([P, 1], F32)
         nc.scalar.activation(out=table_warm[:], in_=eps[:], func=ACT.Abs_reciprocal_sqrt)
 
         load_hid(0, 2)
-        nc.sync.dma_start(out=rows[0:1, :], in_=b2.unsqueeze(0))
-        nc.sync.dma_start(out=node_rows[0:NODES, :], in_=nodes)
-        load_planes(W2_scales, 0, MD)
-        for h in range(MD // BANK):
-            nc.sync.dma_start(
-                out=w2_sb[:, :, 4 * BANK * h : 4 * BANK * (h + 1)].bitcast(I32),
-                in_=W2_words[:, :, BANK * h : BANK * (h + 1), :].rearrange("g p n t -> p g (n t)").bitcast(I32),
-            )
+        nc.sync.dma_start(out=node_rows[0:NODES, 0:HD], in_=nodes)
+        nc.sync.dma_start(out=node_rows[0:NODES, HD : 2 * HD], in_=nodes)
+        nc.sync.dma_start(out=b2_cols[:], in_=b2.rearrange("(g p t) -> p g t", g=GROUPS, t=PACK))
+        load_planes(w2_raw_scales, W2_scales)
+        load_w2(0)
+        load_w2(1)
+        load_p_ln(0, 2)
+        load_hid(2, 2)
         nc.sync.dma_start(out=rows[1:2, 0:ED], in_=bo.unsqueeze(0))
         nc.sync.dma_start(out=rows[1:2, ED : 2 * ED], in_=ln_out_g.unsqueeze(0))
         nc.sync.dma_start(out=rows[2:3, 0:ED], in_=ln_out_b.unsqueeze(0))
-        load_p_ln(0, 2)
-        load_hid(2, 2)
-        load_p_ln(2, 2)
-        load_planes(Wo_scales, 8, ED)
+        load_planes(wo_scales, Wo_scales)
         nc.sync.dma_start(
             out=wo_sb[:].bitcast(I32), in_=Wo_words.rearrange("g p n t -> p g (n t)").bitcast(I32)
         )
+        load_p_ln(2, 2)
         load_hid(4, 2)
         load_p_ln(4, 4)
         load_hid(6, 2)
 
-        def spread(dst, pick, src):
-            width = dst.shape[1]
-            spread_bank = psum_z.tile([P, BANK], F32, tag="acc")
-            nc.tensor.matmul(out=spread_bank[:, 0:width], lhsT=pick, rhs=src, start=True, stop=True)
-            nc.scalar.copy(out=dst, in_=spread_bank[:, 0:width])
+        def turn_nodes():
+            words = node_rows[:].bitcast(F32)
+            turned = psum_z.tile([P, 4, P], F32, tag="acc")
+            for u in range(2):
+                nc.tensor.transpose(turned[:, u, :], words[:, u : 2 * P : 2], ident[:])
+            nc.scalar.copy(
+                out=x_turned[:].rearrange("p n t -> p (n t)").bitcast(F32).rearrange("p (n u) -> p n u", u=2),
+                in_=turned[:, 0:2, 0:NODES].rearrange("p u n -> p n u"),
+            )
 
-        def pick_row(k):
-            return ident_bf[:, k : k + 1].to_broadcast([P, P])
+        x_words = x_turned[:].rearrange("p n t -> p (n t)").bitcast(F32).rearrange("p (n u) -> p n u", u=2)
+        z_words = z_nodes[:].rearrange("p b n t -> p b (n t)").bitcast(F32).rearrange("p b (i a u) -> p b i a u", a=4, u=2)
 
-        def spread_nodes(r):
-            node_bank = psum_z.tile([P, BANK], F32, tag="acc")
-            nc.tensor.matmul(out=node_bank[:, 0:HD], lhsT=pick_i[:], rhs=node_rows[:], start=True, stop=True)
-            nc.tensor.matmul(out=node_bank[:, HD : 2 * HD], lhsT=pick_j[:, r, :], rhs=node_rows[:], start=True, stop=True)
-            nc.scalar.copy(out=z_in[:, r, 0 : 2 * HD], in_=node_bank[:])
+        def place_x_i(b):
+            nc.vector.tensor_copy(
+                out=z_words[0:64, b], in_=x_words[0:64].unsqueeze(2).to_broadcast([64, NODES, 4, 2])
+            )
+
+        def place_x_j(r):
+            nc.scalar.copy(
+                out=z_words[64:128, r % 3], in_=x_words[64:128, r : NODES : TILES].unsqueeze(1).to_broadcast([64, NODES, 4, 2])
+            )
+
+        def reorder_w2(h):
+            cols = slice(512 * h, 512 * (h + 1))
+            nc.vector.tensor_copy(
+                out=w2_sb[:, :, cols].rearrange("p g (t m) -> p g t m", t=PACK),
+                in_=w2_raw[:, :, cols].rearrange("p g (m t) -> p g t m", t=PACK),
+            )
+            nc.vector.tensor_copy(
+                out=w2_scales[:, cols].rearrange("p (t m) -> p t m", t=PACK),
+                in_=w2_raw_scales[:, cols].rearrange("p (m t) -> p t m", t=PACK),
+            )
 
         ln_rows = [(lnb_bc, 2, 0), (bo_bc, 1, 0), (g_bc, 1, ED)]
 
         def spread_ln_row(n):
             dst, k, first = ln_rows[n]
-            spread(dst[:], pick_row(k), rows[:, first : first + ED])
-
-        def to_k_on_partitions(rows_bf16, grouped):
-            words = rows_bf16.bitcast(F32)
-            turned = psum_t.tile([P, GROUPS, 2, P], F32)
-            for g in range(GROUPS):
-                for u in range(2):
-                    nc.tensor.transpose(turned[:, g, u, :], words[:, 256 * g + u : 256 * (g + 1) : 2], ident[:])
-            nc.scalar.copy(
-                out=grouped[:].bitcast(F32).rearrange("p (g e u) -> p g e u", g=GROUPS, u=2),
-                in_=turned[:].rearrange("p g u e -> p g e u"),
-            )
-
-        def quantise(grouped, codes, scales):
-            nc.vector.quantize_mx(
-                out=codes.rearrange("p g e -> p (g e)").bitcast(FP8X4),
-                scales=scales.rearrange("p g e -> p (g e)"),
-                in_=grouped[:],
-            )
+            spread_bank = psum_z.tile([P, ED], F32, tag="acc")
+            pick = ident_bf[:, k : k + 1].to_broadcast([P, P])
+            nc.tensor.matmul(out=spread_bank[:], lhsT=pick, rhs=rows[:, first : first + ED], start=True, stop=True)
+            nc.scalar.copy(out=dst[:], in_=spread_bank[:])
 
         live = {}
 
         def turn_hid(r):
-            hid_grouped = work.tile([P, GROUPS * P * 4], BF16, align_bytes=64)
-            to_k_on_partitions(hid_sb[:, r, :], hid_grouped)
+            words = hid_sb[:, r, :].bitcast(F32)
+            turned = psum_t.tile([P, GROUPS, 2, P], F32)
+            for g in range(GROUPS):
+                for u in range(2):
+                    nc.tensor.transpose(turned[:, g, u, :], words[:, 256 * g + u : 256 * (g + 1) : 2], ident[:])
+            live["turned", r] = turned
+
+        def group_hid(r):
+            hid_grouped = work.tile([P, GROUPS * P * PACK], BF16, align_bytes=64)
+            nc.scalar.copy(
+                out=hid_grouped[:].bitcast(F32).rearrange("p (g e u) -> p g e u", g=GROUPS, u=2),
+                in_=live["turned", r][:].rearrange("p g u e -> p g e u"),
+            )
             live["hid_grouped", r] = hid_grouped
 
         def quantise_hid(r):
-            quantise(live["hid_grouped", r], hid_codes[:, r], hid_scales[:, r])
+            nc.vector.quantize_mx(
+                out=hid_codes[:, r].rearrange("p g e -> p (g e)").bitcast(FP8X4),
+                scales=hid_scales[:, r].rearrange("p g e -> p (g e)"),
+                in_=live["hid_grouped", r][:],
+            )
+
+        def turn_p_ln(r):
+            words = p_ln_sb[:, r, :].bitcast(F32)
+            turned = psum_p.tile([P, 2, P], F32)
+            for u in range(2):
+                nc.tensor.transpose(turned[:, u, :], words[:, u : 2 * P : 2], ident[:])
+            live["p_turned", r] = turned
 
         def first_matmul(r):
-            for h in range(MD // BANK):
-                y = psum_y.tile([P, BANK], F32)
-                for g in range(GROUPS):
-                    nc.tensor.matmul_mx(
-                        out=y[:],
-                        lhsT=hid_codes[:, r, g, :].bitcast(FP8X4),
-                        lhsT_scale=hid_scales[:, r, g, :],
-                        rhs=w2_sb[:, g, 4 * BANK * h : 4 * BANK * (h + 1)].bitcast(FP8X4),
-                        rhs_scale=planes[4 * g : P, BANK * h : BANK * (h + 1)],
-                        start=(g == 0),
-                        stop=(g == GROUPS - 1),
-                    )
+            for h in range(2):
+                y = psum_y.tile([P, PACK, P], F32)
+                for t in range(PACK):
+                    cols = slice(P * (PACK * h + t), P * (PACK * h + t + 1))
+                    for g in range(GROUPS):
+                        nc.tensor.matmul_mx(
+                            out=y[:, t, :],
+                            lhsT=w2_sb[:, g, cols].bitcast(FP8X4),
+                            lhsT_scale=w2_scales[4 * g : P, cols],
+                            rhs=hid_codes[:, r, g, :].bitcast(FP8X4),
+                            rhs_scale=hid_scales[:, r, g, :],
+                            start=(g == 0),
+                            stop=(g == GROUPS - 1),
+                        )
                 live["y", r, h] = y
 
-        def add_b2(r):
-            pre = work.tile([P, MD], F32)
-            for h in range(MD // BANK):
-                cols = slice(BANK * h, BANK * (h + 1))
-                nc.vector.tensor_tensor(out=pre[:, cols], in0=live["y", r, h][:], in1=b2_bc[:, cols], op=ALU.add)
-            live["pre", r] = pre
+        def relu(r):
+            for h in range(2):
+                m = work.tile([P, PACK, P], F32, tag="m%d" % h)
+                for t in range(PACK):
+                    nc.scalar.activation(
+                        out=m[:, t, :], in_=live["y", r, h][:, t, :], func=ACT.Relu, bias=b2_cols[:, h, t : t + 1], scale=1.0
+                    )
+                live["m", r, h] = m
 
-        def relu_add_z(r):
-            pre = live["pre", r]
-            s_sb = work.tile([P, MD], BF16)
-            nc.vector.scalar_tensor_tensor(
-                out=s_sb[:], in0=pre[:], scalar=0.0, in1=z_in[:, r, :], op0=ALU.max, op1=ALU.add
+        def add_z(r):
+            s_grouped = work.tile([P, GROUPS, P, PACK], BF16, align_bytes=64)
+            nc.vector.tensor_tensor(
+                out=s_grouped[:, 0], in0=live["m", r, 0][:].rearrange("p t e -> p e t"), in1=z_nodes[:, r % 3], op=ALU.add
             )
-            live["s", r] = s_sb
-
-        def turn_s(r):
-            s_grouped = work.tile([P, GROUPS * P * 4], BF16, align_bytes=64)
-            to_k_on_partitions(live["s", r][:], s_grouped)
+            nc.vector.tensor_tensor(
+                out=s_grouped[:, 1].rearrange("p e (u v) -> p e u v", u=2),
+                in0=live["m", r, 1][:].rearrange("p (u v) e -> p e u v", u=2),
+                in1=live["p_turned", r][:].bitcast(BF16).rearrange("p u (e v) -> p e u v", v=2),
+                op=ALU.add,
+            )
             live["s_grouped", r] = s_grouped
 
         def quantise_s(r):
             s_codes = work.tile([P, GROUPS, P], U32, align_bytes=64)
             s_scales = work.tile([P, GROUPS, P], U8, align_bytes=64)
-            quantise(live["s_grouped", r], s_codes[:], s_scales[:])
+            nc.vector.quantize_mx(
+                out=s_codes[:].rearrange("p g e -> p (g e)").bitcast(FP8X4),
+                scales=s_scales[:].rearrange("p g e -> p (g e)"),
+                in_=live["s_grouped", r][:].rearrange("p g e t -> p (g e t)"),
+            )
             live["s_codes", r] = s_codes
             live["s_scales", r] = s_scales
 
@@ -221,7 +254,7 @@ def tile_edgeupdaterwrapper_v01_pb_kernel(
                     lhsT=live["s_codes", r][:, g, :].bitcast(FP8X4),
                     lhsT_scale=live["s_scales", r][:, g, :],
                     rhs=wo_sb[:, g, :].bitcast(FP8X4),
-                    rhs_scale=planes[8 + 4 * g : P, 0:ED],
+                    rhs_scale=wo_scales[4 * g : P, :],
                     start=(g == 0),
                     stop=(g == GROUPS - 1),
                 )
@@ -236,17 +269,19 @@ def tile_edgeupdaterwrapper_v01_pb_kernel(
             live["z", r] = z
             live["z_sum", r] = z_sum
 
-        def variance(r):
+        def mean(r):
             neg_mean = stats.tile([P, 1], F32)
             nc.vector.tensor_scalar_mul(out=neg_mean[:], in0=live["z_sum", r][:], scalar1=-1.0 / ED)
+            live["neg_mean", r] = neg_mean
+
+        def variance(r):
             squares = work.tile([P, ED], F32)
             sq_sum = stats.tile([P, 1], F32)
             nc.scalar.activation(
-                out=squares[:], in_=live["z", r][:], func=ACT.Square, bias=neg_mean[:], scale=1.0, accum_out=sq_sum[:]
+                out=squares[:], in_=live["z", r][:], func=ACT.Square, bias=live["neg_mean", r][:], scale=1.0, accum_out=sq_sum[:]
             )
             rstd = stats.tile([P, 1], F32)
             nc.scalar.activation(out=rstd[:], in_=sq_sum[:], func=ACT.Abs_reciprocal_sqrt, bias=eps[:], scale=1.0 / ED)
-            live["neg_mean", r] = neg_mean
             live["rstd", r] = rstd
 
         def centre_times_g(r):
@@ -257,7 +292,7 @@ def tile_edgeupdaterwrapper_v01_pb_kernel(
             live["scaled", r] = scaled
 
         def residual(r):
-            nc.gpsimd.tensor_tensor(out=resid[:, r, :], in0=z_in[:, r, 2 * HD : MD], in1=lnb_bc[:], op=ALU.add)
+            nc.gpsimd.tensor_tensor(out=resid[:, r, :], in0=p_ln_sb[:, r, :], in1=lnb_bc[:], op=ALU.add)
 
         def finish(r):
             result = work.tile([P, ED], F32)
@@ -271,32 +306,46 @@ def tile_edgeupdaterwrapper_v01_pb_kernel(
                 work_of(r)
 
         turn_hid(0)
-        spread(b2_bc[:, 0:BANK], pick_row(0), rows[:, 0:BANK])
-        spread(b2_bc[:, BANK:MD], pick_row(0), rows[:, BANK:MD])
-        turn_hid(1)
+        group_hid(0)
+        turn_nodes()
         quantise_hid(0)
-        first_matmul(0)
-        spread_nodes(0)
+        turn_hid(1)
+        group_hid(1)
+        for b in range(3):
+            place_x_i(b)
+        place_x_j(0)
+        place_x_j(1)
         quantise_hid(1)
-        spread_nodes(1)
+        reorder_w2(0)
+        reorder_w2(1)
+        first_matmul(0)
+        turn_p_ln(0)
         turn_hid(2)
+        first_matmul(1)
+        relu(0)
+        group_hid(2)
+        quantise_hid(2)
+        spread_ln_row(0)
+        for r in range(TILES):
+            residual(r)
 
-        for k in range(TILES + 3):
-            stage(turn_s, k - 1)
-            stage(second_matmul, k - 2)
-            stage(first_matmul, k + 1)
-            stage(spread_nodes, k + 2)
-            stage(turn_hid, k + 3)
-            if k < len(ln_rows):
-                spread_ln_row(k)
+        for k in range(TILES + 2):
+            stage(second_matmul, k - 1)
+            stage(first_matmul, k + 2)
             if k == 0:
-                for r in range(TILES):
-                    residual(r)
-            stage(add_b2, k)
-            stage(relu_add_z, k)
-            stage(add_bo, k - 2)
-            stage(quantise_s, k - 1)
-            stage(variance, k - 2)
-            stage(quantise_hid, k + 2)
-            stage(finish, k - 3)
-            stage(centre_times_g, k - 2)
+                spread_ln_row(1)
+                spread_ln_row(2)
+            stage(relu, k + 1)
+            stage(turn_hid, k + 3)
+            stage(group_hid, k + 3)
+            stage(add_z, k)
+            stage(turn_p_ln, k + 1)
+            stage(add_bo, k - 1)
+            if k + 2 < TILES:
+                place_x_j(k + 2)
+            stage(finish, k - 2)
+            stage(quantise_s, k)
+            stage(mean, k - 1)
+            stage(quantise_hid, k + 3)
+            stage(variance, k - 1)
+            stage(centre_times_g, k - 1)

@@ -42,10 +42,9 @@ def tile_edgeupdaterwrapper_v01_pb_kernel(
         keep = ctx.enter_context(tc.tile_pool(name="keep", bufs=1))
         work = ctx.enter_context(tc.tile_pool(name="work", bufs=3))
         stats = ctx.enter_context(tc.tile_pool(name="stats", bufs=4))
-        psum_t = ctx.enter_context(tc.psum_pool(name="psum_t", bufs=1))
         psum_p = ctx.enter_context(tc.psum_pool(name="psum_p", bufs=1))
         psum_y = ctx.enter_context(tc.psum_pool(name="psum_y", bufs=4))
-        psum_z = ctx.enter_context(tc.psum_pool(name="psum_z", bufs=2))
+        psum_z = ctx.enter_context(tc.psum_pool(name="psum_z", bufs=3))
 
         hid_sb = keep.tile([P, TILES, F], BF16)
         p_ln_sb = keep.tile([P, TILES, ED], BF16)
@@ -70,11 +69,11 @@ def tile_edgeupdaterwrapper_v01_pb_kernel(
         hid_codes = keep.tile([P, TILES, GROUPS, P], U32, align_bytes=64)
         hid_scales = keep.tile([P, TILES, GROUPS, P], U8, align_bytes=64)
 
+        nc.vector.memset(w2_raw_scales[:].bitcast(I32), 0)
         nc.vector.memset(eps[:], EPS)
         nc.vector.memset(node_rows[:].bitcast(I32), 0)
-        nc.vector.memset(w2_raw_scales[:].bitcast(I32), 0)
-        nc.vector.memset(wo_scales[:].bitcast(I32), 0)
         nc.vector.memset(rows[:].bitcast(I32), 0)
+        nc.vector.memset(wo_scales[:].bitcast(I32), 0)
         make_identity(nc, ident[:])
         make_identity(nc, ident_bf[:])
 
@@ -100,18 +99,19 @@ def tile_edgeupdaterwrapper_v01_pb_kernel(
         table_warm = keep.tile([P, 1], F32)
         nc.scalar.activation(out=table_warm[:], in_=eps[:], func=ACT.Abs_reciprocal_sqrt)
 
-        load_hid(0, 2)
-        nc.sync.dma_start(out=node_rows[0:NODES, 0:HD], in_=nodes)
-        nc.sync.dma_start(out=node_rows[0:NODES, HD : 2 * HD], in_=nodes)
-        nc.sync.dma_start(out=b2_cols[:], in_=b2.rearrange("(g p t) -> p g t", g=GROUPS, t=PACK))
         load_planes(w2_raw_scales, W2_scales)
+        load_hid(0, 2)
         load_w2(0)
         load_w2(1)
+        nc.gpsimd.dma_start(
+            out=node_rows[0:NODES, :].rearrange("n (c f) -> n c f", c=2), in_=nodes.unsqueeze(1).to_broadcast([NODES, 2, HD])
+        )
+        nc.gpsimd.dma_start(out=b2_cols[:], in_=b2.rearrange("(g p t) -> p g t", g=GROUPS, t=PACK))
+        nc.gpsimd.dma_start(out=rows[2:3, 0:ED], in_=ln_out_b.unsqueeze(0))
+        nc.gpsimd.dma_start(out=rows[1:2, 0:ED], in_=bo.unsqueeze(0))
+        nc.gpsimd.dma_start(out=rows[1:2, ED : 2 * ED], in_=ln_out_g.unsqueeze(0))
         load_p_ln(0, 2)
         load_hid(2, 2)
-        nc.sync.dma_start(out=rows[1:2, 0:ED], in_=bo.unsqueeze(0))
-        nc.sync.dma_start(out=rows[1:2, ED : 2 * ED], in_=ln_out_g.unsqueeze(0))
-        nc.sync.dma_start(out=rows[2:3, 0:ED], in_=ln_out_b.unsqueeze(0))
         load_planes(wo_scales, Wo_scales)
         nc.sync.dma_start(
             out=wo_sb[:].bitcast(I32), in_=Wo_words.rearrange("g p n t -> p g (n t)").bitcast(I32)
@@ -144,31 +144,37 @@ def tile_edgeupdaterwrapper_v01_pb_kernel(
                 out=z_words[64:128, r % 3], in_=x_words[64:128, r : NODES : TILES].unsqueeze(1).to_broadcast([64, NODES, 4, 2])
             )
 
-        def reorder_w2(h):
+        def reorder_words(h):
             cols = slice(512 * h, 512 * (h + 1))
             nc.vector.tensor_copy(
                 out=w2_sb[:, :, cols].rearrange("p g (t m) -> p g t m", t=PACK),
                 in_=w2_raw[:, :, cols].rearrange("p g (m t) -> p g t m", t=PACK),
             )
+
+        def reorder_scales(h):
+            cols = slice(512 * h, 512 * (h + 1))
             nc.vector.tensor_copy(
                 out=w2_scales[:, cols].rearrange("p (t m) -> p t m", t=PACK),
                 in_=w2_raw_scales[:, cols].rearrange("p (m t) -> p t m", t=PACK),
             )
 
-        ln_rows = [(lnb_bc, 2, 0), (bo_bc, 1, 0), (g_bc, 1, ED)]
+        ln_rows = [(bo_bc, 1, 0), (g_bc, 1, ED), (lnb_bc, 2, 0)]
 
         def spread_ln_row(n):
             dst, k, first = ln_rows[n]
             spread_bank = psum_z.tile([P, ED], F32, tag="acc")
             pick = ident_bf[:, k : k + 1].to_broadcast([P, P])
             nc.tensor.matmul(out=spread_bank[:], lhsT=pick, rhs=rows[:, first : first + ED], start=True, stop=True)
-            nc.scalar.copy(out=dst[:], in_=spread_bank[:])
+            live["spread", n] = spread_bank
+
+        def copy_ln_row(n):
+            nc.vector.tensor_copy(out=ln_rows[n][0][:], in_=live["spread", n][:])
 
         live = {}
 
         def turn_hid(r):
             words = hid_sb[:, r, :].bitcast(F32)
-            turned = psum_t.tile([P, GROUPS, 2, P], F32)
+            turned = psum_z.tile([P, GROUPS, 2, P], F32, tag="acc")
             for g in range(GROUPS):
                 for u in range(2):
                     nc.tensor.transpose(turned[:, g, u, :], words[:, 256 * g + u : 256 * (g + 1) : 2], ident[:])
@@ -196,31 +202,38 @@ def tile_edgeupdaterwrapper_v01_pb_kernel(
                 nc.tensor.transpose(turned[:, u, :], words[:, u : 2 * P : 2], ident[:])
             live["p_turned", r] = turned
 
+        def first_matmul_half(r, h):
+            y = psum_y.tile([P, PACK, P], F32)
+            for t in range(PACK):
+                cols = slice(P * (PACK * h + t), P * (PACK * h + t + 1))
+                for g in range(GROUPS):
+                    nc.tensor.matmul_mx(
+                        out=y[:, t, :],
+                        lhsT=w2_sb[:, g, cols].bitcast(FP8X4),
+                        lhsT_scale=w2_scales[4 * g : P, cols],
+                        rhs=hid_codes[:, r, g, :].bitcast(FP8X4),
+                        rhs_scale=hid_scales[:, r, g, :],
+                        start=(g == 0),
+                        stop=(g == GROUPS - 1),
+                    )
+            live["y", r, h] = y
+
         def first_matmul(r):
             for h in range(2):
-                y = psum_y.tile([P, PACK, P], F32)
-                for t in range(PACK):
-                    cols = slice(P * (PACK * h + t), P * (PACK * h + t + 1))
-                    for g in range(GROUPS):
-                        nc.tensor.matmul_mx(
-                            out=y[:, t, :],
-                            lhsT=w2_sb[:, g, cols].bitcast(FP8X4),
-                            lhsT_scale=w2_scales[4 * g : P, cols],
-                            rhs=hid_codes[:, r, g, :].bitcast(FP8X4),
-                            rhs_scale=hid_scales[:, r, g, :],
-                            start=(g == 0),
-                            stop=(g == GROUPS - 1),
-                        )
-                live["y", r, h] = y
+                first_matmul_half(r, h)
+
+        def relu_half(r, h):
+            m = work.tile([P, PACK, P], F32, tag="m%d" % h)
+            for t in range(PACK):
+                nc.scalar.activation(
+                    out=m[:, t, :], in_=live["y", r, h][:, t, :], func=ACT.Relu, bias=b2_cols[:, h, t : t + 1], scale=1.0
+                )
+            live["m", r, h] = m
 
         def relu(r):
             for h in range(2):
-                m = work.tile([P, PACK, P], F32, tag="m%d" % h)
-                for t in range(PACK):
-                    nc.scalar.activation(
-                        out=m[:, t, :], in_=live["y", r, h][:, t, :], func=ACT.Relu, bias=b2_cols[:, h, t : t + 1], scale=1.0
-                    )
-                live["m", r, h] = m
+                if ("m", r, h) not in live:
+                    relu_half(r, h)
 
         def add_z(r):
             s_grouped = work.tile([P, GROUPS, P, PACK], BF16, align_bytes=64)
@@ -307,45 +320,51 @@ def tile_edgeupdaterwrapper_v01_pb_kernel(
 
         turn_hid(0)
         group_hid(0)
-        turn_nodes()
-        quantise_hid(0)
         turn_hid(1)
         group_hid(1)
+        reorder_scales(0)
+        reorder_scales(1)
+        reorder_words(0)
+        quantise_hid(0)
+        reorder_words(1)
+        quantise_hid(1)
+        first_matmul_half(0, 0)
+        turn_nodes()
         for b in range(3):
             place_x_i(b)
         place_x_j(0)
-        place_x_j(1)
-        quantise_hid(1)
-        reorder_w2(0)
-        reorder_w2(1)
-        first_matmul(0)
+        relu_half(0, 0)
+        first_matmul_half(0, 1)
         turn_p_ln(0)
+        relu_half(0, 1)
         turn_hid(2)
-        first_matmul(1)
-        relu(0)
-        group_hid(2)
-        quantise_hid(2)
         spread_ln_row(0)
-        for r in range(TILES):
-            residual(r)
+        first_matmul(1)
+        group_hid(2)
+        place_x_j(1)
 
         for k in range(TILES + 2):
             stage(second_matmul, k - 1)
-            stage(first_matmul, k + 2)
-            if k == 0:
-                spread_ln_row(1)
-                spread_ln_row(2)
             stage(relu, k + 1)
             stage(turn_hid, k + 3)
-            stage(group_hid, k + 3)
             stage(add_z, k)
             stage(turn_p_ln, k + 1)
-            stage(add_bo, k - 1)
+            stage(group_hid, k + 3)
+            stage(quantise_hid, k + 2)
+            if k == 0:
+                copy_ln_row(0)
+                spread_ln_row(1)
+                copy_ln_row(1)
+                spread_ln_row(2)
+                copy_ln_row(2)
+                for r in range(TILES):
+                    residual(r)
+            stage(first_matmul, k + 2)
             if k + 2 < TILES:
                 place_x_j(k + 2)
-            stage(finish, k - 2)
+            stage(add_bo, k - 1)
             stage(quantise_s, k)
             stage(mean, k - 1)
-            stage(quantise_hid, k + 3)
             stage(variance, k - 1)
+            stage(finish, k - 2)
             stage(centre_times_g, k - 1)

@@ -43,7 +43,8 @@ def tile_edgeupdaterwrapper_v01_pb_kernel(
         work = ctx.enter_context(tc.tile_pool(name="work", bufs=3))
         stats = ctx.enter_context(tc.tile_pool(name="stats", bufs=4))
         psum_p = ctx.enter_context(tc.psum_pool(name="psum_p", bufs=1))
-        psum_y = ctx.enter_context(tc.psum_pool(name="psum_y", bufs=4))
+        psum_y = ctx.enter_context(tc.psum_pool(name="psum_y", bufs=3))
+        psum_r = ctx.enter_context(tc.psum_pool(name="psum_r", bufs=1))
         psum_z = ctx.enter_context(tc.psum_pool(name="psum_z", bufs=3))
 
         hid_sb = keep.tile([P, TILES, F], BF16)
@@ -62,8 +63,6 @@ def tile_edgeupdaterwrapper_v01_pb_kernel(
         ident_bf = keep.tile([P, P], BF16)
         bo_bc = keep.tile([P, ED], BF16)
         g_bc = keep.tile([P, ED], BF16)
-        lnb_bc = keep.tile([P, ED], BF16)
-        resid = keep.tile([P, TILES, ED], F32)
         ident = keep.tile([P, P], F32)
         eps = keep.tile([P, 1], F32)
         hid_codes = keep.tile([P, TILES, GROUPS, P], U32, align_bytes=64)
@@ -99,8 +98,8 @@ def tile_edgeupdaterwrapper_v01_pb_kernel(
         table_warm = keep.tile([P, 1], F32)
         nc.scalar.activation(out=table_warm[:], in_=eps[:], func=ACT.Abs_reciprocal_sqrt)
 
-        load_planes(w2_raw_scales, W2_scales)
         load_hid(0, 2)
+        load_planes(w2_raw_scales, W2_scales)
         load_w2(0)
         load_w2(1)
         nc.gpsimd.dma_start(
@@ -158,7 +157,7 @@ def tile_edgeupdaterwrapper_v01_pb_kernel(
                 in_=w2_raw_scales[:, cols].rearrange("p (m t) -> p t m", t=PACK),
             )
 
-        ln_rows = [(bo_bc, 1, 0), (g_bc, 1, ED), (lnb_bc, 2, 0)]
+        ln_rows = [(bo_bc, 1, 0), (g_bc, 1, ED)]
 
         def spread_ln_row(n):
             dst, k, first = ln_rows[n]
@@ -305,12 +304,17 @@ def tile_edgeupdaterwrapper_v01_pb_kernel(
             live["scaled", r] = scaled
 
         def residual(r):
-            nc.gpsimd.tensor_tensor(out=resid[:, r, :], in0=p_ln_sb[:, r, :], in1=lnb_bc[:], op=ALU.add)
+            resid = psum_r.tile([P, ED], F32)
+            nc.tensor.matmul(out=resid[:], lhsT=ident_bf[:], rhs=p_ln_sb[:, r, :], start=True, stop=False)
+            nc.tensor.matmul(
+                out=resid[:], lhsT=ident_bf[:, 2:3].to_broadcast([P, P]), rhs=rows[:, 0:ED], start=False, stop=True
+            )
+            live["resid", r] = resid
 
         def finish(r):
             result = work.tile([P, ED], F32)
             nc.vector.scalar_tensor_tensor(
-                out=result[:], in0=live["scaled", r][:], scalar=live["rstd", r][:], in1=resid[:, r, :], op0=ALU.mult, op1=ALU.add
+                out=result[:], in0=live["scaled", r][:], scalar=live["rstd", r][:], in1=live["resid", r][:], op0=ALU.mult, op1=ALU.add
             )
             nc.sync.dma_start(out=out_rows[:, r, :], in_=result[:])
 
@@ -339,6 +343,7 @@ def tile_edgeupdaterwrapper_v01_pb_kernel(
         relu_half(0, 1)
         turn_hid(2)
         spread_ln_row(0)
+        spread_ln_row(1)
         first_matmul(1)
         group_hid(2)
         place_x_j(1)
@@ -353,12 +358,8 @@ def tile_edgeupdaterwrapper_v01_pb_kernel(
             stage(quantise_hid, k + 2)
             if k == 0:
                 copy_ln_row(0)
-                spread_ln_row(1)
                 copy_ln_row(1)
-                spread_ln_row(2)
-                copy_ln_row(2)
-                for r in range(TILES):
-                    residual(r)
+            stage(residual, k - 2)
             stage(first_matmul, k + 2)
             if k + 2 < TILES:
                 place_x_j(k + 2)

@@ -55,12 +55,13 @@ def tile_edgeupdaterwrapper_v01_pb_kernel(
         w2_scales = keep.tile([P, MD], U8, align_bytes=64)
         wo_sb = keep.tile([P, GROUPS, 4 * ED], U8, align_bytes=64)
         wo_scales = keep.tile([P, ED], U8, align_bytes=64)
-        rows = keep.tile([P, 2 * ED], BF16)
+        rows = keep.tile([P, 3 * ED], BF16)
         node_rows = keep.tile([P, 2 * HD], BF16)
         b2_cols = keep.tile([P, GROUPS, PACK], BF16)
         x_turned = keep.tile([P, NODES, PACK], BF16)
         z_nodes = keep.tile([P, 3, P, PACK], BF16)
         ident_bf = keep.tile([P, P], BF16)
+        pick_row = keep.tile([P, P], BF16)
         bo_bc = keep.tile([P, ED], BF16)
         g_bc = keep.tile([P, ED], BF16)
         ident = keep.tile([P, P], F32)
@@ -74,7 +75,9 @@ def tile_edgeupdaterwrapper_v01_pb_kernel(
         nc.vector.memset(rows[:].bitcast(I32), 0)
         nc.vector.memset(wo_scales[:].bitcast(I32), 0)
         make_identity(nc, ident[:])
-        make_identity(nc, ident_bf[:])
+        nc.vector.tensor_copy(out=ident_bf[:], in_=ident[:])
+
+        nc.vector.tensor_copy(out=pick_row[:], in_=ident[:, 0:1].to_broadcast([P, P]))
 
         def load_hid(first, count):
             nc.sync.dma_start(out=hid_sb[:, first : first + count, :], in_=hid_rows[:, first : first + count, :])
@@ -106,11 +109,10 @@ def tile_edgeupdaterwrapper_v01_pb_kernel(
             out=node_rows[0:NODES, :].rearrange("n (c f) -> n c f", c=2), in_=nodes.unsqueeze(1).to_broadcast([NODES, 2, HD])
         )
         nc.gpsimd.dma_start(out=b2_cols[:], in_=b2.rearrange("(g p t) -> p g t", g=GROUPS, t=PACK))
-        nc.gpsimd.dma_start(out=rows[2:3, 0:ED], in_=ln_out_b.unsqueeze(0))
-        nc.gpsimd.dma_start(out=rows[1:2, 0:ED], in_=bo.unsqueeze(0))
-        nc.gpsimd.dma_start(out=rows[1:2, ED : 2 * ED], in_=ln_out_g.unsqueeze(0))
         load_p_ln(0, 2)
         load_hid(2, 2)
+        for n, row in enumerate((bo, ln_out_g, ln_out_b)):
+            nc.sync.dma_start(out=rows[0:1, ED * n : ED * (n + 1)], in_=row.unsqueeze(0))
         load_planes(wo_scales, Wo_scales)
         nc.sync.dma_start(
             out=wo_sb[:].bitcast(I32), in_=Wo_words.rearrange("g p n t -> p g (n t)").bitcast(I32)
@@ -157,17 +159,15 @@ def tile_edgeupdaterwrapper_v01_pb_kernel(
                 in_=w2_raw_scales[:, cols].rearrange("p (m t) -> p t m", t=PACK),
             )
 
-        ln_rows = [(bo_bc, 1, 0), (g_bc, 1, ED)]
+        ln_rows = [bo_bc, g_bc]
 
         def spread_ln_row(n):
-            dst, k, first = ln_rows[n]
             spread_bank = psum_z.tile([P, ED], F32, tag="acc")
-            pick = ident_bf[:, k : k + 1].to_broadcast([P, P])
-            nc.tensor.matmul(out=spread_bank[:], lhsT=pick, rhs=rows[:, first : first + ED], start=True, stop=True)
+            nc.tensor.matmul(out=spread_bank[:], lhsT=pick_row[:], rhs=rows[:, ED * n : ED * (n + 1)], start=True, stop=True)
             live["spread", n] = spread_bank
 
         def copy_ln_row(n):
-            nc.vector.tensor_copy(out=ln_rows[n][0][:], in_=live["spread", n][:])
+            nc.vector.tensor_copy(out=ln_rows[n][:], in_=live["spread", n][:])
 
         live = {}
 
@@ -237,7 +237,10 @@ def tile_edgeupdaterwrapper_v01_pb_kernel(
         def add_z(r):
             s_grouped = work.tile([P, GROUPS, P, PACK], BF16, align_bytes=64)
             nc.vector.tensor_tensor(
-                out=s_grouped[:, 0], in0=live["m", r, 0][:].rearrange("p t e -> p e t"), in1=z_nodes[:, r % 3], op=ALU.add
+                out=s_grouped[:, 0].rearrange("p (c i) t -> p c t i", i=4),
+                in0=live["m", r, 0][:].rearrange("p t (c i) -> p c t i", i=4),
+                in1=z_nodes[:, r % 3].rearrange("p (c i) t -> p c t i", i=4),
+                op=ALU.add,
             )
             nc.vector.tensor_tensor(
                 out=s_grouped[:, 1].rearrange("p e (u v) -> p e u v", u=2),
@@ -307,7 +310,7 @@ def tile_edgeupdaterwrapper_v01_pb_kernel(
             resid = psum_r.tile([P, ED], F32)
             nc.tensor.matmul(out=resid[:], lhsT=ident_bf[:], rhs=p_ln_sb[:, r, :], start=True, stop=False)
             nc.tensor.matmul(
-                out=resid[:], lhsT=ident_bf[:, 2:3].to_broadcast([P, P]), rhs=rows[:, 0:ED], start=False, stop=True
+                out=resid[:], lhsT=pick_row[:], rhs=rows[:, 2 * ED : 3 * ED], start=False, stop=True
             )
             live["resid", r] = resid
 

@@ -16,6 +16,8 @@ P = 128
 NODES = 32
 EDGES = NODES * NODES
 TILES = EDGES // P
+PAIRS = TILES // 2
+W = 2 * P
 HD = 256
 ED = 512
 F = 1024
@@ -40,12 +42,12 @@ def tile_edgeupdaterwrapper_v01_pb_kernel(
     with ExitStack() as ctx:
         ctx.enter_context(tc.manual_schedule())
         keep = ctx.enter_context(tc.tile_pool(name="keep", bufs=1))
-        work = ctx.enter_context(tc.tile_pool(name="work", bufs=3))
+        work = ctx.enter_context(tc.tile_pool(name="work", bufs=2))
+        tiles = ctx.enter_context(tc.tile_pool(name="tiles", bufs=4))
         stats = ctx.enter_context(tc.tile_pool(name="stats", bufs=4))
         psum_p = ctx.enter_context(tc.psum_pool(name="psum_p", bufs=1))
         psum_y = ctx.enter_context(tc.psum_pool(name="psum_y", bufs=3))
-        psum_r = ctx.enter_context(tc.psum_pool(name="psum_r", bufs=1))
-        psum_z = ctx.enter_context(tc.psum_pool(name="psum_z", bufs=3))
+        psum_z = ctx.enter_context(tc.psum_pool(name="psum_z", bufs=4))
 
         hid_sb = keep.tile([P, TILES, F], BF16)
         p_ln_sb = keep.tile([P, TILES, ED], BF16)
@@ -59,15 +61,15 @@ def tile_edgeupdaterwrapper_v01_pb_kernel(
         node_rows = keep.tile([P, 2 * HD], BF16)
         b2_cols = keep.tile([P, GROUPS, PACK], BF16)
         x_turned = keep.tile([P, NODES, PACK], BF16)
-        z_nodes = keep.tile([P, 3, P, PACK], BF16)
+        z_nodes = keep.tile([P, 2, 2, P, PACK], BF16)
         ident_bf = keep.tile([P, P], BF16)
         pick_row = keep.tile([P, P], BF16)
         bo_bc = keep.tile([P, ED], BF16)
         g_bc = keep.tile([P, ED], BF16)
         ident = keep.tile([P, P], F32)
         eps = keep.tile([P, 1], F32)
-        hid_codes = keep.tile([P, TILES, GROUPS, P], U32, align_bytes=64)
-        hid_scales = keep.tile([P, TILES, GROUPS, P], U8, align_bytes=64)
+        hid_codes = keep.tile([P, PAIRS, GROUPS, W], U32, align_bytes=64)
+        hid_scales = keep.tile([P, PAIRS, GROUPS, W], U8, align_bytes=64)
 
         nc.vector.memset(w2_raw_scales[:].bitcast(I32), 0)
         nc.vector.memset(eps[:], EPS)
@@ -133,17 +135,21 @@ def tile_edgeupdaterwrapper_v01_pb_kernel(
             )
 
         x_words = x_turned[:].rearrange("p n t -> p (n t)").bitcast(F32).rearrange("p (n u) -> p n u", u=2)
-        z_words = z_nodes[:].rearrange("p b n t -> p b (n t)").bitcast(F32).rearrange("p b (i a u) -> p b i a u", a=4, u=2)
+        z_words = z_nodes[:].rearrange("p f b n t -> p f b (n t)").bitcast(F32).rearrange("p f b (i a u) -> p f b i a u", a=4, u=2)
 
-        def place_x_i(b):
-            nc.vector.tensor_copy(
-                out=z_words[0:64, b], in_=x_words[0:64].unsqueeze(2).to_broadcast([64, NODES, 4, 2])
-            )
+        def place_x_i(f):
+            for b in range(2):
+                nc.vector.tensor_copy(
+                    out=z_words[0:64, f, b], in_=x_words[0:64].unsqueeze(2).to_broadcast([64, NODES, 4, 2])
+                )
 
-        def place_x_j(r):
-            nc.scalar.copy(
-                out=z_words[64:128, r % 3], in_=x_words[64:128, r : NODES : TILES].unsqueeze(1).to_broadcast([64, NODES, 4, 2])
-            )
+        def place_x_j(q):
+            for b in range(2):
+                r = 2 * q + b
+                nc.scalar.copy(
+                    out=z_words[64:128, q % 2, b],
+                    in_=x_words[64:128, r : NODES : TILES].unsqueeze(1).to_broadcast([64, NODES, 4, 2]),
+                )
 
         def reorder_words(h):
             cols = slice(512 * h, 512 * (h + 1))
@@ -171,103 +177,104 @@ def tile_edgeupdaterwrapper_v01_pb_kernel(
 
         live = {}
 
-        def turn_hid(r):
-            words = hid_sb[:, r, :].bitcast(F32)
-            turned = psum_z.tile([P, GROUPS, 2, P], F32, tag="acc")
-            for g in range(GROUPS):
-                for u in range(2):
-                    nc.tensor.transpose(turned[:, g, u, :], words[:, 256 * g + u : 256 * (g + 1) : 2], ident[:])
-            live["turned", r] = turned
-
-        def group_hid(r):
-            hid_grouped = work.tile([P, GROUPS * P * PACK], BF16, align_bytes=64)
-            nc.scalar.copy(
-                out=hid_grouped[:].bitcast(F32).rearrange("p (g e u) -> p g e u", g=GROUPS, u=2),
-                in_=live["turned", r][:].rearrange("p g u e -> p g e u"),
-            )
-            live["hid_grouped", r] = hid_grouped
-
-        def quantise_hid(r):
-            nc.vector.quantize_mx(
-                out=hid_codes[:, r].rearrange("p g e -> p (g e)").bitcast(FP8X4),
-                scales=hid_scales[:, r].rearrange("p g e -> p (g e)"),
-                in_=live["hid_grouped", r][:],
-            )
-
-        def turn_p_ln(r):
-            words = p_ln_sb[:, r, :].bitcast(F32)
-            turned = psum_p.tile([P, 2, P], F32)
-            for u in range(2):
-                nc.tensor.transpose(turned[:, u, :], words[:, u : 2 * P : 2], ident[:])
-            live["p_turned", r] = turned
-
-        def first_matmul_half(r, h):
-            y = psum_y.tile([P, PACK, P], F32)
-            for t in range(PACK):
-                cols = slice(P * (PACK * h + t), P * (PACK * h + t + 1))
+        def turn_hid(q):
+            for b in range(2):
+                words = hid_sb[:, 2 * q + b, :].bitcast(F32)
+                turned = psum_z.tile([P, GROUPS, 2, P], F32, tag="acc")
                 for g in range(GROUPS):
-                    nc.tensor.matmul_mx(
-                        out=y[:, t, :],
-                        lhsT=w2_sb[:, g, cols].bitcast(FP8X4),
-                        lhsT_scale=w2_scales[4 * g : P, cols],
-                        rhs=hid_codes[:, r, g, :].bitcast(FP8X4),
-                        rhs_scale=hid_scales[:, r, g, :],
-                        start=(g == 0),
-                        stop=(g == GROUPS - 1),
-                    )
-            live["y", r, h] = y
+                    for u in range(2):
+                        nc.tensor.transpose(turned[:, g, u, :], words[:, 256 * g + u : 256 * (g + 1) : 2], ident[:])
+                live["turned", q, b] = turned
 
-        def first_matmul(r):
-            for h in range(2):
-                first_matmul_half(r, h)
+        def group_hid(q):
+            hid_grouped = work.tile([P, GROUPS, W * PACK], BF16, align_bytes=64)
+            for b in range(2):
+                nc.scalar.copy(
+                    out=hid_grouped[:].bitcast(F32).rearrange("p g (b e u) -> p g b e u", b=2, u=2)[:, :, b],
+                    in_=live["turned", q, b][:].rearrange("p g u e -> p g e u"),
+                )
+            live["hid_grouped", q] = hid_grouped
 
-        def relu_half(r, h):
-            m = work.tile([P, PACK, P], F32, tag="m%d" % h)
+        def quantise_hid(q):
+            for g in range(GROUPS):
+                nc.vector.quantize_mx(
+                    out=hid_codes[:, q, g, :].bitcast(FP8X4),
+                    scales=hid_scales[:, q, g, :],
+                    in_=live["hid_grouped", q][:, g, :],
+                )
+
+        def turn_p_ln(q):
+            turned = psum_p.tile([P, 2, W], F32)
+            for b in range(2):
+                words = p_ln_sb[:, 2 * q + b, :].bitcast(F32)
+                for u in range(2):
+                    nc.tensor.transpose(turned[:, u, P * b : P * (b + 1)], words[:, u : 2 * P : 2], ident[:])
+            live["p_turned", q] = turned
+
+        def first_matmul(q, h):
+            for th in range(2):
+                y = psum_y.tile([P, 2, W], F32)
+                for tl in range(2):
+                    t = 2 * th + tl
+                    cols = slice(P * (PACK * h + t), P * (PACK * h + t + 1))
+                    for g in range(GROUPS):
+                        nc.tensor.matmul_mx(
+                            out=y[:, tl, :],
+                            lhsT=w2_sb[:, g, cols].bitcast(FP8X4),
+                            lhsT_scale=w2_scales[4 * g : P, cols],
+                            rhs=hid_codes[:, q, g, :].bitcast(FP8X4),
+                            rhs_scale=hid_scales[:, q, g, :],
+                            start=(g == 0),
+                            stop=(g == GROUPS - 1),
+                        )
+                live["y", q, h, th] = y
+
+        def relu(q, h):
+            m = work.tile([P, PACK, W], F32, tag="m%d" % h)
             for t in range(PACK):
                 nc.scalar.activation(
-                    out=m[:, t, :], in_=live["y", r, h][:, t, :], func=ACT.Relu, bias=b2_cols[:, h, t : t + 1], scale=1.0
+                    out=m[:, t, :], in_=live["y", q, h, t // 2][:, t % 2, :], func=ACT.Relu, bias=b2_cols[:, h, t : t + 1], scale=1.0
                 )
-            live["m", r, h] = m
+            live["m", q, h] = m
 
-        def relu(r):
-            for h in range(2):
-                if ("m", r, h) not in live:
-                    relu_half(r, h)
-
-        def add_z(r):
-            s_grouped = work.tile([P, GROUPS, P, PACK], BF16, align_bytes=64)
+        def add_x(q):
+            s_grouped = work.tile([P, GROUPS, W, PACK], BF16, align_bytes=64)
             nc.vector.tensor_tensor(
                 out=s_grouped[:, 0].rearrange("p (c i) t -> p c t i", i=4),
-                in0=live["m", r, 0][:].rearrange("p t (c i) -> p c t i", i=4),
-                in1=z_nodes[:, r % 3].rearrange("p (c i) t -> p c t i", i=4),
+                in0=live["m", q, 0][:].rearrange("p t (c i) -> p c t i", i=4),
+                in1=z_nodes[:, q % 2].rearrange("p b n t -> p (b n) t").rearrange("p (c i) t -> p c t i", i=4),
                 op=ALU.add,
             )
-            nc.vector.tensor_tensor(
-                out=s_grouped[:, 1].rearrange("p e (u v) -> p e u v", u=2),
-                in0=live["m", r, 1][:].rearrange("p (u v) e -> p e u v", u=2),
-                in1=live["p_turned", r][:].bitcast(BF16).rearrange("p u (e v) -> p e u v", v=2),
-                op=ALU.add,
-            )
-            live["s_grouped", r] = s_grouped
+            live["s_grouped", q] = s_grouped
 
-        def quantise_s(r):
-            s_codes = work.tile([P, GROUPS, P], U32, align_bytes=64)
-            s_scales = work.tile([P, GROUPS, P], U8, align_bytes=64)
-            nc.vector.quantize_mx(
-                out=s_codes[:].rearrange("p g e -> p (g e)").bitcast(FP8X4),
-                scales=s_scales[:].rearrange("p g e -> p (g e)"),
-                in_=live["s_grouped", r][:].rearrange("p g e t -> p (g e t)"),
+        def add_p_ln(q):
+            nc.vector.tensor_tensor(
+                out=live["s_grouped", q][:, 1].rearrange("p e (u v) -> p e u v", u=2),
+                in0=live["m", q, 1][:].rearrange("p (u v) e -> p e u v", u=2),
+                in1=live["p_turned", q][:].bitcast(BF16).rearrange("p u (e v) -> p e u v", v=2),
+                op=ALU.add,
             )
-            live["s_codes", r] = s_codes
-            live["s_scales", r] = s_scales
+
+        def quantise_s(q):
+            s_codes = work.tile([P, GROUPS, W], U32, align_bytes=64)
+            s_scales = work.tile([P, GROUPS, W], U8, align_bytes=64)
+            for g in range(GROUPS):
+                nc.vector.quantize_mx(
+                    out=s_codes[:, g, :].bitcast(FP8X4),
+                    scales=s_scales[:, g, :],
+                    in_=live["s_grouped", q][:, g].rearrange("p e t -> p (e t)"),
+                )
+            live["s_codes", q] = s_codes
+            live["s_scales", q] = s_scales
 
         def second_matmul(r):
+            rows_of_pair = slice(P * (r % 2), P * (r % 2 + 1))
             acc = psum_z.tile([P, ED], F32, tag="acc")
             for g in range(GROUPS):
                 nc.tensor.matmul_mx(
                     out=acc[:],
-                    lhsT=live["s_codes", r][:, g, :].bitcast(FP8X4),
-                    lhsT_scale=live["s_scales", r][:, g, :],
+                    lhsT=live["s_codes", r // 2][:, g, rows_of_pair].bitcast(FP8X4),
+                    lhsT_scale=live["s_scales", r // 2][:, g, rows_of_pair],
                     rhs=wo_sb[:, g, :].bitcast(FP8X4),
                     rhs_scale=wo_scales[4 * g : P, :],
                     start=(g == 0),
@@ -275,100 +282,113 @@ def tile_edgeupdaterwrapper_v01_pb_kernel(
                 )
             live["acc", r] = acc
 
-        def add_bo(r):
-            z = work.tile([P, ED], F32)
-            z_sum = stats.tile([P, 1], F32)
-            nc.vector.scalar_tensor_tensor(
-                out=z[:], in0=live["acc", r][:], scalar=1.0, in1=bo_bc[:], op0=ALU.mult, op1=ALU.add, accum_out=z_sum[:]
-            )
-            live["z", r] = z
-            live["z_sum", r] = z_sum
+        def add_bo(q):
+            z_sum = stats.tile([P, 2], F32)
+            for b in range(2):
+                z = tiles.tile([P, ED], F32)
+                nc.vector.scalar_tensor_tensor(
+                    out=z[:], in0=live["acc", 2 * q + b][:], scalar=1.0, in1=bo_bc[:], op0=ALU.mult, op1=ALU.add,
+                    accum_out=z_sum[:, b : b + 1],
+                )
+                live["z", 2 * q + b] = z
+            live["z_sum", q] = z_sum
 
-        def mean(r):
-            neg_mean = stats.tile([P, 1], F32)
-            nc.vector.tensor_scalar_mul(out=neg_mean[:], in0=live["z_sum", r][:], scalar1=-1.0 / ED)
-            live["neg_mean", r] = neg_mean
+        def mean(q):
+            neg_mean = stats.tile([P, 2], F32)
+            nc.vector.tensor_scalar_mul(out=neg_mean[:], in0=live["z_sum", q][:], scalar1=-1.0 / ED)
+            live["neg_mean", q] = neg_mean
 
-        def variance(r):
-            squares = work.tile([P, ED], F32)
-            sq_sum = stats.tile([P, 1], F32)
-            nc.scalar.activation(
-                out=squares[:], in_=live["z", r][:], func=ACT.Square, bias=live["neg_mean", r][:], scale=1.0, accum_out=sq_sum[:]
-            )
-            rstd = stats.tile([P, 1], F32)
+        def variance(q):
+            sq_sum = stats.tile([P, 2], F32)
+            for b in range(2):
+                squares = tiles.tile([P, ED], F32)
+                nc.scalar.activation(
+                    out=squares[:], in_=live["z", 2 * q + b][:], func=ACT.Square, bias=live["neg_mean", q][:, b : b + 1],
+                    scale=1.0, accum_out=sq_sum[:, b : b + 1],
+                )
+            rstd = stats.tile([P, 2], F32)
             nc.scalar.activation(out=rstd[:], in_=sq_sum[:], func=ACT.Abs_reciprocal_sqrt, bias=eps[:], scale=1.0 / ED)
-            live["rstd", r] = rstd
+            live["rstd", q] = rstd
 
         def centre_times_g(r):
-            scaled = work.tile([P, ED], F32)
+            scaled = tiles.tile([P, ED], F32)
             nc.vector.scalar_tensor_tensor(
-                out=scaled[:], in0=live["z", r][:], scalar=live["neg_mean", r][:], in1=g_bc[:], op0=ALU.add, op1=ALU.mult
+                out=scaled[:], in0=live["z", r][:], scalar=live["neg_mean", r // 2][:, r % 2 : r % 2 + 1], in1=g_bc[:],
+                op0=ALU.add, op1=ALU.mult,
             )
             live["scaled", r] = scaled
 
         def residual(r):
-            resid = psum_r.tile([P, ED], F32)
+            resid = psum_z.tile([P, ED], F32, tag="acc")
             nc.tensor.matmul(out=resid[:], lhsT=ident_bf[:], rhs=p_ln_sb[:, r, :], start=True, stop=False)
-            nc.tensor.matmul(
-                out=resid[:], lhsT=pick_row[:], rhs=rows[:, 2 * ED : 3 * ED], start=False, stop=True
-            )
+            nc.tensor.matmul(out=resid[:], lhsT=pick_row[:], rhs=rows[:, 2 * ED : 3 * ED], start=False, stop=True)
             live["resid", r] = resid
 
         def finish(r):
-            result = work.tile([P, ED], F32)
+            result = tiles.tile([P, ED], F32)
             nc.vector.scalar_tensor_tensor(
-                out=result[:], in0=live["scaled", r][:], scalar=live["rstd", r][:], in1=live["resid", r][:], op0=ALU.mult, op1=ALU.add
+                out=result[:], in0=live["scaled", r][:], scalar=live["rstd", r // 2][:, r % 2 : r % 2 + 1], in1=live["resid", r][:],
+                op0=ALU.mult, op1=ALU.add,
             )
             nc.sync.dma_start(out=out_rows[:, r, :], in_=result[:])
 
-        def stage(work_of, r):
-            if 0 <= r < TILES:
-                work_of(r)
+        def stage(work_of, q, *args):
+            if 0 <= q < PAIRS:
+                work_of(q, *args)
+
+        def both(work_of, q):
+            if 0 <= q < PAIRS:
+                work_of(2 * q)
+                work_of(2 * q + 1)
 
         turn_hid(0)
         group_hid(0)
-        turn_hid(1)
-        group_hid(1)
-        reorder_scales(0)
-        reorder_scales(1)
+        for h in range(2):
+            reorder_scales(h)
         reorder_words(0)
         quantise_hid(0)
         reorder_words(1)
-        quantise_hid(1)
-        first_matmul_half(0, 0)
+        first_matmul(0, 0)
         turn_nodes()
-        for b in range(3):
-            place_x_i(b)
+        for f in range(2):
+            place_x_i(f)
         place_x_j(0)
-        relu_half(0, 0)
-        first_matmul_half(0, 1)
+        relu(0, 0)
+        first_matmul(0, 1)
         turn_p_ln(0)
-        relu_half(0, 1)
-        turn_hid(2)
-        spread_ln_row(0)
-        spread_ln_row(1)
-        first_matmul(1)
-        group_hid(2)
+        turn_hid(1)
+        relu(0, 1)
+        group_hid(1)
+        for n in range(2):
+            spread_ln_row(n)
         place_x_j(1)
 
-        for k in range(TILES + 2):
-            stage(second_matmul, k - 1)
-            stage(relu, k + 1)
-            stage(turn_hid, k + 3)
-            stage(add_z, k)
-            stage(turn_p_ln, k + 1)
-            stage(group_hid, k + 3)
-            stage(quantise_hid, k + 2)
-            if k == 0:
-                copy_ln_row(0)
-                copy_ln_row(1)
-            stage(residual, k - 2)
-            stage(first_matmul, k + 2)
-            if k + 2 < TILES:
-                place_x_j(k + 2)
-            stage(add_bo, k - 1)
-            stage(quantise_s, k)
-            stage(mean, k - 1)
-            stage(variance, k - 1)
-            stage(finish, k - 2)
-            stage(centre_times_g, k - 1)
+        for q in range(PAIRS + 1):
+            if q > 0:
+                stage(turn_hid, q + 2)
+                stage(group_hid, q + 2)
+            stage(add_x, q)
+            stage(add_p_ln, q)
+            if q == 0:
+                quantise_hid(1)
+            stage(quantise_s, q)
+            stage(first_matmul, q + 1, 0)
+            stage(relu, q + 1, 0)
+            both(residual, q - 1)
+            both(second_matmul, q)
+            stage(first_matmul, q + 1, 1)
+            if q + 2 < PAIRS:
+                place_x_j(q + 2)
+            stage(relu, q + 1, 1)
+            stage(turn_p_ln, q + 1)
+            if q == 0:
+                for n in range(2):
+                    copy_ln_row(n)
+                turn_hid(2)
+                group_hid(2)
+            both(centre_times_g, q - 1)
+            both(finish, q - 1)
+            stage(add_bo, q)
+            stage(quantise_hid, q + 2)
+            stage(mean, q)
+            stage(variance, q)

@@ -16,8 +16,7 @@ P = 128
 NODES = 32
 EDGES = NODES * NODES
 TILES = EDGES // P
-PAIRS = TILES // 2
-W = 2 * P
+CHUNKS = ((0, 1), (1, 2), (3, 2), (5, 2), (7, 1))
 HD = 256
 ED = 512
 F = 1024
@@ -25,6 +24,7 @@ MD = 1024
 GROUPS = 2
 PACK = 4
 EPS = 1e-5
+BANK = 512
 
 FLOPS = 2 * EDGES * F * MD + 2 * EDGES * MD * ED
 
@@ -46,8 +46,9 @@ def tile_edgeupdaterwrapper_v01_pb_kernel(
         tiles = ctx.enter_context(tc.tile_pool(name="tiles", bufs=4))
         stats = ctx.enter_context(tc.tile_pool(name="stats", bufs=4))
         psum_p = ctx.enter_context(tc.psum_pool(name="psum_p", bufs=1))
-        psum_y = ctx.enter_context(tc.psum_pool(name="psum_y", bufs=3))
-        psum_z = ctx.enter_context(tc.psum_pool(name="psum_z", bufs=4))
+        psum_y = ctx.enter_context(tc.psum_pool(name="psum_y", bufs=2))
+        psum_t = ctx.enter_context(tc.psum_pool(name="psum_t", bufs=3))
+        psum_z = ctx.enter_context(tc.psum_pool(name="psum_z", bufs=2))
 
         hid_sb = keep.tile([P, TILES, F], BF16)
         p_ln_sb = keep.tile([P, TILES, ED], BF16)
@@ -61,15 +62,13 @@ def tile_edgeupdaterwrapper_v01_pb_kernel(
         node_rows = keep.tile([P, 2 * HD], BF16)
         b2_cols = keep.tile([P, GROUPS, PACK], BF16)
         x_turned = keep.tile([P, NODES, PACK], BF16)
-        z_nodes = keep.tile([P, 2, 2, P, PACK], BF16)
+        z_nodes = keep.tile([P, 2, 2 * P, PACK], BF16)
         ident_bf = keep.tile([P, P], BF16)
         pick_row = keep.tile([P, P], BF16)
         bo_bc = keep.tile([P, ED], BF16)
         g_bc = keep.tile([P, ED], BF16)
         ident = keep.tile([P, P], F32)
         eps = keep.tile([P, 1], F32)
-        hid_codes = keep.tile([P, PAIRS, GROUPS, W], U32, align_bytes=64)
-        hid_scales = keep.tile([P, PAIRS, GROUPS, W], U8, align_bytes=64)
 
         nc.vector.memset(w2_raw_scales[:].bitcast(I32), 0)
         nc.vector.memset(eps[:], EPS)
@@ -103,30 +102,31 @@ def tile_edgeupdaterwrapper_v01_pb_kernel(
         table_warm = keep.tile([P, 1], F32)
         nc.scalar.activation(out=table_warm[:], in_=eps[:], func=ACT.Abs_reciprocal_sqrt)
 
-        load_hid(0, 2)
+        nc.scalar.dma_start(out=b2_cols[:], in_=b2.rearrange("(g p t) -> p g t", g=GROUPS, t=PACK))
+        load_hid(0, 1)
         load_planes(w2_raw_scales, W2_scales)
-        load_w2(0)
-        load_w2(1)
-        nc.gpsimd.dma_start(
+        nc.sync.dma_start(
             out=node_rows[0:NODES, :].rearrange("n (c f) -> n c f", c=2), in_=nodes.unsqueeze(1).to_broadcast([NODES, 2, HD])
         )
-        nc.gpsimd.dma_start(out=b2_cols[:], in_=b2.rearrange("(g p t) -> p g t", g=GROUPS, t=PACK))
-        load_p_ln(0, 2)
-        load_hid(2, 2)
+        load_w2(0)
+        load_w2(1)
+        load_p_ln(0, 1)
+        load_hid(1, 2)
         for n, row in enumerate((bo, ln_out_g, ln_out_b)):
             nc.sync.dma_start(out=rows[0:1, ED * n : ED * (n + 1)], in_=row.unsqueeze(0))
-        load_planes(wo_scales, Wo_scales)
+        load_p_ln(1, 2)
         nc.sync.dma_start(
             out=wo_sb[:].bitcast(I32), in_=Wo_words.rearrange("g p n t -> p g (n t)").bitcast(I32)
         )
-        load_p_ln(2, 2)
-        load_hid(4, 2)
-        load_p_ln(4, 4)
-        load_hid(6, 2)
+        load_planes(wo_scales, Wo_scales)
+        load_hid(3, 2)
+        load_p_ln(3, 2)
+        load_hid(5, 3)
+        load_p_ln(5, 3)
 
         def turn_nodes():
             words = node_rows[:].bitcast(F32)
-            turned = psum_z.tile([P, 4, P], F32, tag="acc")
+            turned = psum_t.tile([P, 4, P], F32, name="nodes_turned", tag="t")
             for u in range(2):
                 nc.tensor.transpose(turned[:, u, :], words[:, u : 2 * P : 2], ident[:])
             nc.scalar.copy(
@@ -135,20 +135,19 @@ def tile_edgeupdaterwrapper_v01_pb_kernel(
             )
 
         x_words = x_turned[:].rearrange("p n t -> p (n t)").bitcast(F32).rearrange("p (n u) -> p n u", u=2)
-        z_words = z_nodes[:].rearrange("p f b n t -> p f b (n t)").bitcast(F32).rearrange("p f b (i a u) -> p f b i a u", a=4, u=2)
+        z_words = z_nodes[:].rearrange("p f n t -> p f (n t)").bitcast(F32).rearrange("p f (b i a u) -> p f b i a u", b=2, a=4, u=2)
 
-        def place_x_i(f):
-            for b in range(2):
-                nc.vector.tensor_copy(
-                    out=z_words[0:64, f, b], in_=x_words[0:64].unsqueeze(2).to_broadcast([64, NODES, 4, 2])
-                )
+        def place_x_i(f, b):
+            nc.vector.tensor_copy(
+                out=z_words[0:64, f, b], in_=x_words[0:64].unsqueeze(2).to_broadcast([64, NODES, 4, 2])
+            )
 
-        def place_x_j(q):
-            for b in range(2):
-                r = 2 * q + b
+        def place_x_j(c):
+            first, count = CHUNKS[c]
+            for b in range(count):
                 nc.scalar.copy(
-                    out=z_words[64:128, q % 2, b],
-                    in_=x_words[64:128, r : NODES : TILES].unsqueeze(1).to_broadcast([64, NODES, 4, 2]),
+                    out=z_words[64:128, c % 2, b],
+                    in_=x_words[64:128, first + b : NODES : TILES].unsqueeze(1).to_broadcast([64, NODES, 4, 2]),
                 )
 
         def reorder_words(h):
@@ -177,104 +176,110 @@ def tile_edgeupdaterwrapper_v01_pb_kernel(
 
         live = {}
 
-        def turn_hid(q):
-            for b in range(2):
-                words = hid_sb[:, 2 * q + b, :].bitcast(F32)
-                turned = psum_z.tile([P, GROUPS, 2, P], F32, tag="acc")
+        def turn_hid(c):
+            first, count = CHUNKS[c]
+            for b in range(count):
+                words = hid_sb[:, first + b, :].bitcast(F32)
+                turned = psum_t.tile([P, GROUPS, 2, P], F32, name="hid_turned", tag="t")
                 for g in range(GROUPS):
                     for u in range(2):
                         nc.tensor.transpose(turned[:, g, u, :], words[:, 256 * g + u : 256 * (g + 1) : 2], ident[:])
-                live["turned", q, b] = turned
+                live["turned", c, b] = turned
 
-        def group_hid(q):
-            hid_grouped = work.tile([P, GROUPS, W * PACK], BF16, align_bytes=64)
-            for b in range(2):
+        def group_hid(c):
+            count = CHUNKS[c][1]
+            hid_grouped = work.tile([P, GROUPS, count * P * PACK], BF16, align_bytes=64, name="hid_grouped%d" % count)
+            for b in range(count):
                 nc.scalar.copy(
-                    out=hid_grouped[:].bitcast(F32).rearrange("p g (b e u) -> p g b e u", b=2, u=2)[:, :, b],
-                    in_=live["turned", q, b][:].rearrange("p g u e -> p g e u"),
+                    out=hid_grouped[:].bitcast(F32).rearrange("p g (b e u) -> p g b e u", b=count, u=2)[:, :, b],
+                    in_=live["turned", c, b][:].rearrange("p g u e -> p g e u"),
                 )
-            live["hid_grouped", q] = hid_grouped
+            live["hid_grouped", c] = hid_grouped
 
-        def quantise_hid(q):
+        def quantise(grouped, codes, scales):
             for g in range(GROUPS):
-                nc.vector.quantize_mx(
-                    out=hid_codes[:, q, g, :].bitcast(FP8X4),
-                    scales=hid_scales[:, q, g, :],
-                    in_=live["hid_grouped", q][:, g, :],
-                )
+                nc.vector.quantize_mx(out=codes[:, g, :].bitcast(FP8X4), scales=scales[:, g, :], in_=grouped[:, g])
 
-        def turn_p_ln(q):
-            turned = psum_p.tile([P, 2, W], F32)
-            for b in range(2):
-                words = p_ln_sb[:, 2 * q + b, :].bitcast(F32)
+        def quantise_hid(c):
+            count = CHUNKS[c][1]
+            hid_codes = work.tile([P, GROUPS, count * P], U32, align_bytes=64, name="hid_codes%d" % count)
+            hid_scales = work.tile([P, GROUPS, count * P], U8, align_bytes=64, name="hid_scales%d" % count)
+            quantise(live["hid_grouped", c], hid_codes, hid_scales)
+            live["hid_codes", c] = hid_codes
+            live["hid_scales", c] = hid_scales
+
+        def turn_p_ln(c):
+            first, count = CHUNKS[c]
+            turned = psum_p.tile([P, 2, count * P], F32, name="p_turned%d" % count, tag="p_turned")
+            for b in range(count):
+                words = p_ln_sb[:, first + b, :].bitcast(F32)
                 for u in range(2):
                     nc.tensor.transpose(turned[:, u, P * b : P * (b + 1)], words[:, u : 2 * P : 2], ident[:])
-            live["p_turned", q] = turned
+            live["p_turned", c] = turned
 
-        def first_matmul(q, h):
-            for th in range(2):
-                y = psum_y.tile([P, 2, W], F32)
-                for tl in range(2):
-                    t = 2 * th + tl
-                    cols = slice(P * (PACK * h + t), P * (PACK * h + t + 1))
-                    for g in range(GROUPS):
-                        nc.tensor.matmul_mx(
-                            out=y[:, tl, :],
-                            lhsT=w2_sb[:, g, cols].bitcast(FP8X4),
-                            lhsT_scale=w2_scales[4 * g : P, cols],
-                            rhs=hid_codes[:, q, g, :].bitcast(FP8X4),
-                            rhs_scale=hid_scales[:, q, g, :],
-                            start=(g == 0),
-                            stop=(g == GROUPS - 1),
-                        )
-                live["y", q, h, th] = y
+        def first_matmul(c, h):
+            width = CHUNKS[c][1] * P
+            in_bank = BANK // width
+            for t in range(PACK):
+                if t % in_bank == 0:
+                    y = psum_y.tile([P, in_bank, width], F32, name="y%d" % width, tag="y")
+                cols = slice(P * (PACK * h + t), P * (PACK * h + t + 1))
+                for g in range(GROUPS):
+                    nc.tensor.matmul_mx(
+                        out=y[:, t % in_bank, :],
+                        lhsT=w2_sb[:, g, cols].bitcast(FP8X4),
+                        lhsT_scale=w2_scales[4 * g : P, cols],
+                        rhs=live["hid_codes", c][:, g, :].bitcast(FP8X4),
+                        rhs_scale=live["hid_scales", c][:, g, :],
+                        start=(g == 0),
+                        stop=(g == GROUPS - 1),
+                    )
+                live["y", c, h, t] = y[:, t % in_bank, :]
 
-        def relu(q, h):
-            m = work.tile([P, PACK, W], F32, tag="m%d" % h)
+        def relu(c, h):
+            width = CHUNKS[c][1] * P
+            m = work.tile([P, PACK, width], F32, name="m%d_%d" % (h, width))
             for t in range(PACK):
                 nc.scalar.activation(
-                    out=m[:, t, :], in_=live["y", q, h, t // 2][:, t % 2, :], func=ACT.Relu, bias=b2_cols[:, h, t : t + 1], scale=1.0
+                    out=m[:, t, :], in_=live["y", c, h, t], func=ACT.Relu, bias=b2_cols[:, h, t : t + 1], scale=1.0
                 )
-            live["m", q, h] = m
+            live["m", c, h] = m
 
-        def add_x(q):
-            s_grouped = work.tile([P, GROUPS, W, PACK], BF16, align_bytes=64)
+        def add_x(c):
+            width = CHUNKS[c][1] * P
+            s_grouped = work.tile([P, GROUPS, width * PACK], BF16, align_bytes=64, name="s_grouped%d" % width)
             nc.vector.tensor_tensor(
-                out=s_grouped[:, 0].rearrange("p (c i) t -> p c t i", i=4),
-                in0=live["m", q, 0][:].rearrange("p t (c i) -> p c t i", i=4),
-                in1=z_nodes[:, q % 2].rearrange("p b n t -> p (b n) t").rearrange("p (c i) t -> p c t i", i=4),
+                out=s_grouped[:, 0].rearrange("p (c i t) -> p c t i", i=4, t=PACK),
+                in0=live["m", c, 0][:].rearrange("p t (c i) -> p c t i", i=4),
+                in1=z_nodes[:, c % 2, 0:width].rearrange("p (c i) t -> p c t i", i=4),
                 op=ALU.add,
             )
-            live["s_grouped", q] = s_grouped
+            live["s_grouped", c] = s_grouped
 
-        def add_p_ln(q):
+        def add_p_ln(c):
             nc.vector.tensor_tensor(
-                out=live["s_grouped", q][:, 1].rearrange("p e (u v) -> p e u v", u=2),
-                in0=live["m", q, 1][:].rearrange("p (u v) e -> p e u v", u=2),
-                in1=live["p_turned", q][:].bitcast(BF16).rearrange("p u (e v) -> p e u v", v=2),
+                out=live["s_grouped", c][:, 1].rearrange("p (e u v) -> p e u v", u=2, v=2),
+                in0=live["m", c, 1][:].rearrange("p (u v) e -> p e u v", u=2),
+                in1=live["p_turned", c][:].bitcast(BF16).rearrange("p u (e v) -> p e u v", v=2),
                 op=ALU.add,
             )
 
-        def quantise_s(q):
-            s_codes = work.tile([P, GROUPS, W], U32, align_bytes=64)
-            s_scales = work.tile([P, GROUPS, W], U8, align_bytes=64)
-            for g in range(GROUPS):
-                nc.vector.quantize_mx(
-                    out=s_codes[:, g, :].bitcast(FP8X4),
-                    scales=s_scales[:, g, :],
-                    in_=live["s_grouped", q][:, g].rearrange("p e t -> p (e t)"),
-                )
-            live["s_codes", q] = s_codes
-            live["s_scales", q] = s_scales
+        def quantise_s(c):
+            width = CHUNKS[c][1] * P
+            s_codes = work.tile([P, GROUPS, width], U32, align_bytes=64, name="s_codes%d" % width)
+            s_scales = work.tile([P, GROUPS, width], U8, align_bytes=64, name="s_scales%d" % width)
+            quantise(live["s_grouped", c], s_codes, s_scales)
+            for b in range(CHUNKS[c][1]):
+                live["s", CHUNKS[c][0] + b] = (s_codes, s_scales, slice(P * b, P * (b + 1)))
 
         def second_matmul(r):
-            rows_of_pair = slice(P * (r % 2), P * (r % 2 + 1))
+            s_codes, s_scales, edges = live["s", r]
             acc = psum_z.tile([P, ED], F32, tag="acc")
             for g in range(GROUPS):
                 nc.tensor.matmul_mx(
                     out=acc[:],
-                    lhsT=live["s_codes", r // 2][:, g, rows_of_pair].bitcast(FP8X4),
-                    lhsT_scale=live["s_scales", r // 2][:, g, rows_of_pair],
+                    lhsT=s_codes[:, g, edges].bitcast(FP8X4),
+                    lhsT_scale=s_scales[:, g, edges],
                     rhs=wo_sb[:, g, :].bitcast(FP8X4),
                     rhs_scale=wo_scales[4 * g : P, :],
                     start=(g == 0),
@@ -282,44 +287,50 @@ def tile_edgeupdaterwrapper_v01_pb_kernel(
                 )
             live["acc", r] = acc
 
-        def add_bo(q):
+        def add_bo(c):
+            first, count = CHUNKS[c]
             z_sum = stats.tile([P, 2], F32)
-            for b in range(2):
+            for b in range(count):
                 z = tiles.tile([P, ED], F32)
                 nc.vector.scalar_tensor_tensor(
-                    out=z[:], in0=live["acc", 2 * q + b][:], scalar=1.0, in1=bo_bc[:], op0=ALU.mult, op1=ALU.add,
+                    out=z[:], in0=live["acc", first + b][:], scalar=1.0, in1=bo_bc[:], op0=ALU.mult, op1=ALU.add,
                     accum_out=z_sum[:, b : b + 1],
                 )
-                live["z", 2 * q + b] = z
-            live["z_sum", q] = z_sum
+                live["z", first + b] = z
+            live["z_sum", c] = z_sum
 
-        def mean(q):
+        def mean(c):
+            first, count = CHUNKS[c]
             neg_mean = stats.tile([P, 2], F32)
-            nc.vector.tensor_scalar_mul(out=neg_mean[:], in0=live["z_sum", q][:], scalar1=-1.0 / ED)
-            live["neg_mean", q] = neg_mean
+            nc.vector.tensor_scalar_mul(out=neg_mean[:, 0:count], in0=live["z_sum", c][:, 0:count], scalar1=-1.0 / ED)
+            for b in range(count):
+                live["neg_mean", first + b] = neg_mean[:, b : b + 1]
 
-        def variance(q):
+        def variance(c):
+            first, count = CHUNKS[c]
             sq_sum = stats.tile([P, 2], F32)
-            for b in range(2):
+            for b in range(count):
                 squares = tiles.tile([P, ED], F32)
                 nc.scalar.activation(
-                    out=squares[:], in_=live["z", 2 * q + b][:], func=ACT.Square, bias=live["neg_mean", q][:, b : b + 1],
+                    out=squares[:], in_=live["z", first + b][:], func=ACT.Square, bias=live["neg_mean", first + b],
                     scale=1.0, accum_out=sq_sum[:, b : b + 1],
                 )
             rstd = stats.tile([P, 2], F32)
-            nc.scalar.activation(out=rstd[:], in_=sq_sum[:], func=ACT.Abs_reciprocal_sqrt, bias=eps[:], scale=1.0 / ED)
-            live["rstd", q] = rstd
+            nc.scalar.activation(
+                out=rstd[:, 0:count], in_=sq_sum[:, 0:count], func=ACT.Abs_reciprocal_sqrt, bias=eps[:], scale=1.0 / ED
+            )
+            for b in range(count):
+                live["rstd", first + b] = rstd[:, b : b + 1]
 
         def centre_times_g(r):
             scaled = tiles.tile([P, ED], F32)
             nc.vector.scalar_tensor_tensor(
-                out=scaled[:], in0=live["z", r][:], scalar=live["neg_mean", r // 2][:, r % 2 : r % 2 + 1], in1=g_bc[:],
-                op0=ALU.add, op1=ALU.mult,
+                out=scaled[:], in0=live["z", r][:], scalar=live["neg_mean", r], in1=g_bc[:], op0=ALU.add, op1=ALU.mult
             )
             live["scaled", r] = scaled
 
         def residual(r):
-            resid = psum_z.tile([P, ED], F32, tag="acc")
+            resid = psum_t.tile([P, ED], F32, tag="t")
             nc.tensor.matmul(out=resid[:], lhsT=ident_bf[:], rhs=p_ln_sb[:, r, :], start=True, stop=False)
             nc.tensor.matmul(out=resid[:], lhsT=pick_row[:], rhs=rows[:, 2 * ED : 3 * ED], start=False, stop=True)
             live["resid", r] = resid
@@ -327,68 +338,67 @@ def tile_edgeupdaterwrapper_v01_pb_kernel(
         def finish(r):
             result = tiles.tile([P, ED], F32)
             nc.vector.scalar_tensor_tensor(
-                out=result[:], in0=live["scaled", r][:], scalar=live["rstd", r // 2][:, r % 2 : r % 2 + 1], in1=live["resid", r][:],
-                op0=ALU.mult, op1=ALU.add,
+                out=result[:], in0=live["scaled", r][:], scalar=live["rstd", r], in1=live["resid", r][:], op0=ALU.mult, op1=ALU.add
             )
             nc.sync.dma_start(out=out_rows[:, r, :], in_=result[:])
 
-        def stage(work_of, q, *args):
-            if 0 <= q < PAIRS:
-                work_of(q, *args)
+        def stage(work_of, c, *args):
+            if 0 <= c < len(CHUNKS):
+                work_of(c, *args)
 
-        def both(work_of, q):
-            if 0 <= q < PAIRS:
-                work_of(2 * q)
-                work_of(2 * q + 1)
+        def each(work_of, c):
+            if 0 <= c < len(CHUNKS):
+                for b in range(CHUNKS[c][1]):
+                    work_of(CHUNKS[c][0] + b)
 
         turn_hid(0)
         group_hid(0)
+        turn_nodes()
         for h in range(2):
             reorder_scales(h)
         reorder_words(0)
         quantise_hid(0)
-        reorder_words(1)
+        place_x_i(0, 0)
         first_matmul(0, 0)
-        turn_nodes()
-        for f in range(2):
-            place_x_i(f)
         place_x_j(0)
         relu(0, 0)
+        reorder_words(1)
         first_matmul(0, 1)
-        turn_p_ln(0)
-        turn_hid(1)
         relu(0, 1)
-        group_hid(1)
-        for n in range(2):
-            spread_ln_row(n)
-        place_x_j(1)
+        turn_p_ln(0)
+        for f, b in ((1, 0), (1, 1), (0, 1)):
+            place_x_i(f, b)
 
-        for q in range(PAIRS + 1):
-            if q > 0:
-                stage(turn_hid, q + 2)
-                stage(group_hid, q + 2)
-            stage(add_x, q)
-            stage(add_p_ln, q)
-            if q == 0:
-                quantise_hid(1)
-            stage(quantise_s, q)
-            stage(first_matmul, q + 1, 0)
-            stage(relu, q + 1, 0)
-            both(residual, q - 1)
-            both(second_matmul, q)
-            stage(first_matmul, q + 1, 1)
-            if q + 2 < PAIRS:
-                place_x_j(q + 2)
-            stage(relu, q + 1, 1)
-            stage(turn_p_ln, q + 1)
-            if q == 0:
+        for c in range(len(CHUNKS) + 2):
+            if c == 0:
+                turn_hid(1)
+                group_hid(1)
+                for n in range(2):
+                    spread_ln_row(n)
+                place_x_j(1)
+            each(residual, c - 2)
+            stage(add_x, c)
+            if c + 2 < len(CHUNKS):
+                place_x_j(c + 2)
+            stage(add_bo, c - 1)
+            if c == 0:
+                stage(add_p_ln, c)
+            stage(quantise_hid, c + 1)
+            stage(first_matmul, c + 1, 0)
+            stage(relu, c + 1, 0)
+            if c > 0:
+                stage(add_p_ln, c)
+            stage(mean, c - 1)
+            stage(quantise_s, c)
+            if c == 0:
                 for n in range(2):
                     copy_ln_row(n)
-                turn_hid(2)
-                group_hid(2)
-            both(centre_times_g, q - 1)
-            both(finish, q - 1)
-            stage(add_bo, q)
-            stage(quantise_hid, q + 2)
-            stage(mean, q)
-            stage(variance, q)
+            each(centre_times_g, c - 1)
+            each(finish, c - 2)
+            each(second_matmul, c)
+            stage(variance, c - 1)
+            stage(turn_hid, c + 2)
+            stage(group_hid, c + 2)
+            stage(first_matmul, c + 1, 1)
+            stage(relu, c + 1, 1)
+            stage(turn_p_ln, c + 1)

@@ -137,8 +137,8 @@ def tile_edgeupdaterwrapper_v01_pb_kernel(
         x_words = x_turned[:].rearrange("p n t -> p (n t)").bitcast(F32).rearrange("p (n u) -> p n u", u=2)
         z_words = z_nodes[:].rearrange("p f n t -> p f (n t)").bitcast(F32).rearrange("p f (b i a u) -> p f b i a u", b=2, a=4, u=2)
 
-        def place_x_i(f, b):
-            nc.vector.tensor_copy(
+        def place_x_i(engine, f, b):
+            engine.tensor_copy(
                 out=z_words[0:64, f, b], in_=x_words[0:64].unsqueeze(2).to_broadcast([64, NODES, 4, 2])
             )
 
@@ -204,17 +204,21 @@ def tile_edgeupdaterwrapper_v01_pb_kernel(
             count = CHUNKS[c][1]
             hid_codes = work.tile([P, GROUPS, count * P], U32, align_bytes=64, name="hid_codes%d" % count)
             hid_scales = work.tile([P, GROUPS, count * P], U8, align_bytes=64, name="hid_scales%d" % count)
-            quantise(live["hid_grouped", c], hid_codes, hid_scales)
+            nc.vector.quantize_mx(
+                out=hid_codes[:].rearrange("p g e -> p (g e)").bitcast(FP8X4),
+                scales=hid_scales[:].rearrange("p g e -> p (g e)"),
+                in_=live["hid_grouped", c][:].rearrange("p g k -> p (g k)"),
+            )
             live["hid_codes", c] = hid_codes
             live["hid_scales", c] = hid_scales
 
         def turn_p_ln(c):
             first, count = CHUNKS[c]
-            turned = psum_p.tile([P, 2, count * P], F32, name="p_turned%d" % count, tag="p_turned")
+            turned = psum_p.tile([P, count * P, 2], F32, name="p_turned%d" % count, tag="p_turned")
             for b in range(count):
                 words = p_ln_sb[:, first + b, :].bitcast(F32)
                 for u in range(2):
-                    nc.tensor.transpose(turned[:, u, P * b : P * (b + 1)], words[:, u : 2 * P : 2], ident[:])
+                    nc.tensor.transpose(turned[:, P * b : P * (b + 1), u], words[:, u : 2 * P : 2], ident[:])
             live["p_turned", c] = turned
 
         def first_matmul(c, h):
@@ -248,7 +252,8 @@ def tile_edgeupdaterwrapper_v01_pb_kernel(
         def add_x(c):
             width = CHUNKS[c][1] * P
             s_grouped = work.tile([P, GROUPS, width * PACK], BF16, align_bytes=64, name="s_grouped%d" % width)
-            nc.vector.tensor_tensor(
+            engine = nc.gpsimd if c in (4,) else nc.vector
+            engine.tensor_tensor(
                 out=s_grouped[:, 0].rearrange("p (c i t) -> p c t i", i=4, t=PACK),
                 in0=live["m", c, 0][:].rearrange("p t (c i) -> p c t i", i=4),
                 in1=z_nodes[:, c % 2, 0:width].rearrange("p (c i) t -> p c t i", i=4),
@@ -258,9 +263,9 @@ def tile_edgeupdaterwrapper_v01_pb_kernel(
 
         def add_p_ln(c):
             nc.vector.tensor_tensor(
-                out=live["s_grouped", c][:, 1].rearrange("p (e u v) -> p e u v", u=2, v=2),
-                in0=live["m", c, 1][:].rearrange("p (u v) e -> p e u v", u=2),
-                in1=live["p_turned", c][:].bitcast(BF16).rearrange("p u (e v) -> p e u v", v=2),
+                out=live["s_grouped", c][:, 1].rearrange("p (c i t) -> p c t i", i=4, t=PACK),
+                in0=live["m", c, 1][:].rearrange("p t (c i) -> p c t i", i=4),
+                in1=live["p_turned", c][:].bitcast(BF16).rearrange("p (c i) t -> p c t i", i=4),
                 op=ALU.add,
             )
 
@@ -302,7 +307,9 @@ def tile_edgeupdaterwrapper_v01_pb_kernel(
         def mean(c):
             first, count = CHUNKS[c]
             neg_mean = stats.tile([P, 2], F32)
-            nc.vector.tensor_scalar_mul(out=neg_mean[:, 0:count], in0=live["z_sum", c][:, 0:count], scalar1=-1.0 / ED)
+            nc.gpsimd.tensor_scalar(
+                out=neg_mean[:, 0:count], in0=live["z_sum", c][:, 0:count], scalar1=-1.0 / ED, scalar2=0.0, op0=ALU.mult, op1=ALU.add
+            )
             for b in range(count):
                 live["neg_mean", first + b] = neg_mean[:, b : b + 1]
 
@@ -321,8 +328,31 @@ def tile_edgeupdaterwrapper_v01_pb_kernel(
             )
             for b in range(count):
                 live["rstd", first + b] = rstd[:, b : b + 1]
+            if shared_norm(first):
+                shift = stats.tile([P, 1], F32)
+                nc.scalar.activation(out=shift[:], in_=live["neg_mean", first], func=ACT.Copy, scale=live["rstd", first])
+                normed = tiles.tile([P, ED], F32)
+                nc.scalar.activation(
+                    out=normed[:], in_=live["z", first][:], func=ACT.Identity, bias=shift[:], scale=live["rstd", first]
+                )
+                live["normed", first] = normed
+
+        def shared_norm(r):
+            return any(r == first for first, count in CHUNKS[1:3])
+
+        def times_g(r, c):
+            if shared_norm(r):
+                if c < len(CHUNKS):
+                    scaled = live["m", c, 0][:].rearrange("p t e -> p (t e)")[:, 0:ED]
+                else:
+                    last = tiles.tile([P, ED], F32)
+                    scaled = last[:]
+                nc.gpsimd.tensor_tensor(out=scaled, in0=live["normed", r][:], in1=g_bc[:], op=ALU.mult)
+                live["scaled", r] = scaled
 
         def centre_times_g(r):
+            if shared_norm(r):
+                return
             scaled = tiles.tile([P, ED], F32)
             nc.vector.scalar_tensor_tensor(
                 out=scaled[:], in0=live["z", r][:], scalar=live["neg_mean", r], in1=g_bc[:], op0=ALU.add, op1=ALU.mult
@@ -337,9 +367,12 @@ def tile_edgeupdaterwrapper_v01_pb_kernel(
 
         def finish(r):
             result = tiles.tile([P, ED], F32)
-            nc.vector.scalar_tensor_tensor(
-                out=result[:], in0=live["scaled", r][:], scalar=live["rstd", r], in1=live["resid", r][:], op0=ALU.mult, op1=ALU.add
-            )
+            if shared_norm(r):
+                nc.vector.tensor_tensor(out=result[:], in0=live["scaled", r], in1=live["resid", r][:], op=ALU.add)
+            else:
+                nc.vector.scalar_tensor_tensor(
+                    out=result[:], in0=live["scaled", r][:], scalar=live["rstd", r], in1=live["resid", r][:], op0=ALU.mult, op1=ALU.add
+                )
             nc.sync.dma_start(out=out_rows[:, r, :], in_=result[:])
 
         def stage(work_of, c, *args):
@@ -358,7 +391,7 @@ def tile_edgeupdaterwrapper_v01_pb_kernel(
             reorder_scales(h)
         reorder_words(0)
         quantise_hid(0)
-        place_x_i(0, 0)
+        place_x_i(nc.vector, 0, 0)
         first_matmul(0, 0)
         place_x_j(0)
         relu(0, 0)
@@ -367,7 +400,7 @@ def tile_edgeupdaterwrapper_v01_pb_kernel(
         relu(0, 1)
         turn_p_ln(0)
         for f, b in ((1, 0), (1, 1), (0, 1)):
-            place_x_i(f, b)
+            place_x_i(nc.gpsimd, f, b)
 
         for c in range(len(CHUNKS) + 2):
             if c == 0:
@@ -380,6 +413,8 @@ def tile_edgeupdaterwrapper_v01_pb_kernel(
             stage(add_x, c)
             if c + 2 < len(CHUNKS):
                 place_x_j(c + 2)
+            if 0 <= c - 2 < len(CHUNKS):
+                times_g(CHUNKS[c - 2][0], c)
             stage(add_bo, c - 1)
             if c == 0:
                 stage(add_p_ln, c)

@@ -102,7 +102,6 @@ def tile_edgeupdaterwrapper_v01_pb_kernel(
         table_warm = keep.tile([P, 1], F32)
         nc.scalar.activation(out=table_warm[:], in_=eps[:], func=ACT.Abs_reciprocal_sqrt)
 
-        nc.scalar.dma_start(out=b2_cols[:], in_=b2.rearrange("(g p t) -> p g t", g=GROUPS, t=PACK))
         load_hid(0, 1)
         load_planes(w2_raw_scales, W2_scales)
         nc.sync.dma_start(
@@ -110,6 +109,7 @@ def tile_edgeupdaterwrapper_v01_pb_kernel(
         )
         load_w2(0)
         load_w2(1)
+        nc.scalar.dma_start(out=b2_cols[:], in_=b2.rearrange("(g p t) -> p g t", g=GROUPS, t=PACK))
         load_p_ln(0, 1)
         load_hid(1, 2)
         for n, row in enumerate((bo, ln_out_g, ln_out_b)):

from contextlib import ExitStack

import concourse.mybir as mybir
from concourse.masks import make_identity

F32 = mybir.dt.float32
BF16 = mybir.dt.bfloat16
I32 = mybir.dt.int32
U32 = mybir.dt.uint32
U8 = mybir.dt.uint8
FP8X4 = mybir.dt.float8_e4m3fn_x4
ALU = mybir.AluOpType
ACT = mybir.ActivationFunctionType

P = 128
NODES = 32
EDGES = NODES * NODES
TILES = EDGES // P
CHUNKS = ((0, 1), (1, 2), (3, 2), (5, 2), (7, 1))
HD = 256
ED = 512
F = 1024
MD = 1024
GROUPS = 2
PACK = 4
EPS = 1e-5
BANK = 512

FLOPS = 2 * EDGES * F * MD + 2 * EDGES * MD * ED


def tile_edgeupdaterwrapper_v01_pb_kernel(
    tc, hid, x_down, p_ln, W2_words, W2_scales, b2, Wo_words, Wo_scales, bo, ln_out_g, ln_out_b, out
):
    nc = tc.nc

    hid_rows = hid.flatten_outer_dims().rearrange("(p r) f -> p r f", r=TILES)
    p_ln_rows = p_ln.flatten_outer_dims().rearrange("(p r) f -> p r f", r=TILES)
    out_rows = out.flatten_outer_dims().rearrange("(p r) f -> p r f", r=TILES)
    nodes = x_down.flatten_outer_dims()

    with ExitStack() as ctx:
        ctx.enter_context(tc.manual_schedule())
        keep = ctx.enter_context(tc.tile_pool(name="keep", bufs=1))
        work = ctx.enter_context(tc.tile_pool(name="work", bufs=2))
        tiles = ctx.enter_context(tc.tile_pool(name="tiles", bufs=4))
        stats = ctx.enter_context(tc.tile_pool(name="stats", bufs=4))
        psum_p = ctx.enter_context(tc.psum_pool(name="psum_p", bufs=1))
        psum_y = ctx.enter_context(tc.psum_pool(name="psum_y", bufs=2))
        psum_t = ctx.enter_context(tc.psum_pool(name="psum_t", bufs=3))
        psum_z = ctx.enter_context(tc.psum_pool(name="psum_z", bufs=2))

        hid_sb = keep.tile([P, TILES, F], BF16)
        p_ln_sb = keep.tile([P, TILES, ED], BF16)
        w2_raw = keep.tile([P, GROUPS, MD], I32, align_bytes=64)
        w2_raw_scales = keep.tile([P, MD], U8, align_bytes=64)
        w2_sb = keep.tile([P, GROUPS, MD], I32, align_bytes=64)
        w2_scales = keep.tile([P, MD], U8, align_bytes=64)
        wo_sb = keep.tile([P, GROUPS, 4 * ED], U8, align_bytes=64)
        wo_scales = keep.tile([P, ED], U8, align_bytes=64)
        rows = keep.tile([P, 3 * ED], BF16)
        node_rows = keep.tile([P, 2 * HD], BF16)
        b2_cols = keep.tile([P, GROUPS, PACK], BF16)
        x_turned = keep.tile([P, NODES, PACK], BF16)
        z_nodes = keep.tile([P, 2, 2 * P, PACK], BF16)
        ident_bf = keep.tile([P, P], BF16)
        pick_row = keep.tile([P, P], BF16)
        bo_bc = keep.tile([P, ED], BF16)
        g_bc = keep.tile([P, ED], BF16)
        ident = keep.tile([P, P], F32)
        eps = keep.tile([P, 1], F32)

        nc.vector.memset(w2_raw_scales[:].bitcast(I32), 0)
        nc.vector.memset(eps[:], EPS)
        nc.vector.memset(node_rows[:].bitcast(I32), 0)
        nc.vector.memset(rows[:].bitcast(I32), 0)
        nc.vector.memset(wo_scales[:].bitcast(I32), 0)
        make_identity(nc, ident[:])
        nc.vector.tensor_copy(out=ident_bf[:], in_=ident[:])

        nc.vector.tensor_copy(out=pick_row[:], in_=ident[:, 0:1].to_broadcast([P, P]))

        def load_hid(first, count):
            nc.sync.dma_start(out=hid_sb[:, first : first + count, :], in_=hid_rows[:, first : first + count, :])

        def load_p_ln(first, count):
            nc.sync.dma_start(out=p_ln_sb[:, first : first + count, :], in_=p_ln_rows[:, first : first + count, :])

        def load_planes(dst, scales):
            for q in range(4):
                nc.sync.dma_start(
                    out=dst[32 * q : 32 * q + 8, :].bitcast(I32),
                    in_=scales[:, 4 * q : 4 * q + 4, :].bitcast(I32),
                )

        def load_w2(h):
            nc.sync.dma_start(
                out=w2_raw[:, :, 512 * h : 512 * (h + 1)],
                in_=W2_words[:, :, 512 * h : 512 * (h + 1), :].rearrange("g p n t -> p g (n t)").bitcast(I32),
            )

        table_warm = keep.tile([P, 1], F32)
        nc.scalar.activation(out=table_warm[:], in_=eps[:], func=ACT.Abs_reciprocal_sqrt)

        load_hid(0, 1)
        load_planes(w2_raw_scales, W2_scales)
        nc.sync.dma_start(
            out=node_rows[0:NODES, :].rearrange("n (c f) -> n c f", c=2), in_=nodes.unsqueeze(1).to_broadcast([NODES, 2, HD])
        )
        load_w2(0)
        load_w2(1)
        nc.scalar.dma_start(out=b2_cols[:], in_=b2.rearrange("(g p t) -> p g t", g=GROUPS, t=PACK))
        load_p_ln(0, 1)
        load_hid(1, 2)
        for n, row in enumerate((bo, ln_out_g, ln_out_b)):
            nc.sync.dma_start(out=rows[0:1, ED * n : ED * (n + 1)], in_=row.unsqueeze(0))
        load_p_ln(1, 2)
        nc.sync.dma_start(
            out=wo_sb[:].bitcast(I32), in_=Wo_words.rearrange("g p n t -> p g (n t)").bitcast(I32)
        )
        load_planes(wo_scales, Wo_scales)
        load_hid(3, 2)
        load_p_ln(3, 2)
        load_hid(5, 3)
        load_p_ln(5, 3)

        def turn_nodes():
            words = node_rows[:].bitcast(F32)
            turned = psum_t.tile([P, 4, P], F32, name="nodes_turned", tag="t")
            for u in range(2):
                nc.tensor.transpose(turned[:, u, :], words[:, u : 2 * P : 2], ident[:])
            nc.scalar.copy(
                out=x_turned[:].rearrange("p n t -> p (n t)").bitcast(F32).rearrange("p (n u) -> p n u", u=2),
                in_=turned[:, 0:2, 0:NODES].rearrange("p u n -> p n u"),
            )

        x_words = x_turned[:].rearrange("p n t -> p (n t)").bitcast(F32).rearrange("p (n u) -> p n u", u=2)
        z_words = z_nodes[:].rearrange("p f n t -> p f (n t)").bitcast(F32).rearrange("p f (b i a u) -> p f b i a u", b=2, a=4, u=2)

        def place_x_i(engine, f, b):
            engine.tensor_copy(
                out=z_words[0:64, f, b], in_=x_words[0:64].unsqueeze(2).to_broadcast([64, NODES, 4, 2])
            )

        def place_x_j(c):
            first, count = CHUNKS[c]
            for b in range(count):
                nc.scalar.copy(
                    out=z_words[64:128, c % 2, b],
                    in_=x_words[64:128, first + b : NODES : TILES].unsqueeze(1).to_broadcast([64, NODES, 4, 2]),
                )

        def reorder_words(h):
            cols = slice(512 * h, 512 * (h + 1))
            nc.vector.tensor_copy(
                out=w2_sb[:, :, cols].rearrange("p g (t m) -> p g t m", t=PACK),
                in_=w2_raw[:, :, cols].rearrange("p g (m t) -> p g t m", t=PACK),
            )

        def reorder_scales(h):
            cols = slice(512 * h, 512 * (h + 1))
            nc.vector.tensor_copy(
                out=w2_scales[:, cols].rearrange("p (t m) -> p t m", t=PACK),
                in_=w2_raw_scales[:, cols].rearrange("p (m t) -> p t m", t=PACK),
            )

        ln_rows = [bo_bc, g_bc]

        def spread_ln_row(n):
            spread_bank = psum_z.tile([P, ED], F32, tag="acc")
            nc.tensor.matmul(out=spread_bank[:], lhsT=pick_row[:], rhs=rows[:, ED * n : ED * (n + 1)], start=True, stop=True)
            live["spread", n] = spread_bank

        def copy_ln_row(n):
            nc.vector.tensor_copy(out=ln_rows[n][:], in_=live["spread", n][:])

        live = {}

        def turn_hid(c):
            first, count = CHUNKS[c]
            for b in range(count):
                words = hid_sb[:, first + b, :].bitcast(F32)
                turned = psum_t.tile([P, GROUPS, 2, P], F32, name="hid_turned", tag="t")
                for g in range(GROUPS):
                    for u in range(2):
                        nc.tensor.transpose(turned[:, g, u, :], words[:, 256 * g + u : 256 * (g + 1) : 2], ident[:])
                live["turned", c, b] = turned

        def group_hid(c):
            count = CHUNKS[c][1]
            hid_grouped = work.tile([P, GROUPS, count * P * PACK], BF16, align_bytes=64, name="hid_grouped%d" % count)
            for b in range(count):
                nc.scalar.copy(
                    out=hid_grouped[:].bitcast(F32).rearrange("p g (b e u) -> p g b e u", b=count, u=2)[:, :, b],
                    in_=live["turned", c, b][:].rearrange("p g u e -> p g e u"),
                )
            live["hid_grouped", c] = hid_grouped

        def quantise(grouped, codes, scales):
            for g in range(GROUPS):
                nc.vector.quantize_mx(out=codes[:, g, :].bitcast(FP8X4), scales=scales[:, g, :], in_=grouped[:, g])

        def quantise_hid(c):
            count = CHUNKS[c][1]
            hid_codes = work.tile([P, GROUPS, count * P], U32, align_bytes=64, name="hid_codes%d" % count)
            hid_scales = work.tile([P, GROUPS, count * P], U8, align_bytes=64, name="hid_scales%d" % count)
            nc.vector.quantize_mx(
                out=hid_codes[:].rearrange("p g e -> p (g e)").bitcast(FP8X4),
                scales=hid_scales[:].rearrange("p g e -> p (g e)"),
                in_=live["hid_grouped", c][:].rearrange("p g k -> p (g k)"),
            )
            live["hid_codes", c] = hid_codes
            live["hid_scales", c] = hid_scales

        def turn_p_ln(c):
            first, count = CHUNKS[c]
            turned = psum_p.tile([P, count * P, 2], F32, name="p_turned%d" % count, tag="p_turned")
            for b in range(count):
                words = p_ln_sb[:, first + b, :].bitcast(F32)
                for u in range(2):
                    nc.tensor.transpose(turned[:, P * b : P * (b + 1), u], words[:, u : 2 * P : 2], ident[:])
            live["p_turned", c] = turned

        def first_matmul(c, h):
            width = CHUNKS[c][1] * P
            in_bank = BANK // width
            for t in range(PACK):
                if t % in_bank == 0:
                    y = psum_y.tile([P, in_bank, width], F32, name="y%d" % width, tag="y")
                cols = slice(P * (PACK * h + t), P * (PACK * h + t + 1))
                for g in range(GROUPS):
                    nc.tensor.matmul_mx(
                        out=y[:, t % in_bank, :],
                        lhsT=w2_sb[:, g, cols].bitcast(FP8X4),
                        lhsT_scale=w2_scales[4 * g : P, cols],
                        rhs=live["hid_codes", c][:, g, :].bitcast(FP8X4),
                        rhs_scale=live["hid_scales", c][:, g, :],
                        start=(g == 0),
                        stop=(g == GROUPS - 1),
                    )
                live["y", c, h, t] = y[:, t % in_bank, :]

        def relu(c, h):
            width = CHUNKS[c][1] * P
            m = work.tile([P, PACK, width], F32, name="m%d_%d" % (h, width))
            for t in range(PACK):
                nc.scalar.activation(
                    out=m[:, t, :], in_=live["y", c, h, t], func=ACT.Relu, bias=b2_cols[:, h, t : t + 1], scale=1.0
                )
            live["m", c, h] = m

        def add_x(c):
            width = CHUNKS[c][1] * P
            s_grouped = work.tile([P, GROUPS, width * PACK], BF16, align_bytes=64, name="s_grouped%d" % width)
            engine = nc.gpsimd if c in (4,) else nc.vector
            engine.tensor_tensor(
                out=s_grouped[:, 0].rearrange("p (c i t) -> p c t i", i=4, t=PACK),
                in0=live["m", c, 0][:].rearrange("p t (c i) -> p c t i", i=4),
                in1=z_nodes[:, c % 2, 0:width].rearrange("p (c i) t -> p c t i", i=4),
                op=ALU.add,
            )
            live["s_grouped", c] = s_grouped

        def add_p_ln(c):
            nc.vector.tensor_tensor(
                out=live["s_grouped", c][:, 1].rearrange("p (c i t) -> p c t i", i=4, t=PACK),
                in0=live["m", c, 1][:].rearrange("p t (c i) -> p c t i", i=4),
                in1=live["p_turned", c][:].bitcast(BF16).rearrange("p (c i) t -> p c t i", i=4),
                op=ALU.add,
            )

        def quantise_s(c):
            width = CHUNKS[c][1] * P
            s_codes = work.tile([P, GROUPS, width], U32, align_bytes=64, name="s_codes%d" % width)
            s_scales = work.tile([P, GROUPS, width], U8, align_bytes=64, name="s_scales%d" % width)
            quantise(live["s_grouped", c], s_codes, s_scales)
            for b in range(CHUNKS[c][1]):
                live["s", CHUNKS[c][0] + b] = (s_codes, s_scales, slice(P * b, P * (b + 1)))

        def second_matmul(r):
            s_codes, s_scales, edges = live["s", r]
            acc = psum_z.tile([P, ED], F32, tag="acc")
            for g in range(GROUPS):
                nc.tensor.matmul_mx(
                    out=acc[:],
                    lhsT=s_codes[:, g, edges].bitcast(FP8X4),
                    lhsT_scale=s_scales[:, g, edges],
                    rhs=wo_sb[:, g, :].bitcast(FP8X4),
                    rhs_scale=wo_scales[4 * g : P, :],
                    start=(g == 0),
                    stop=(g == GROUPS - 1),
                )
            live["acc", r] = acc

        def add_bo(c):
            first, count = CHUNKS[c]
            z_sum = stats.tile([P, 2], F32)
            for b in range(count):
                z = tiles.tile([P, ED], F32)
                nc.vector.scalar_tensor_tensor(
                    out=z[:], in0=live["acc", first + b][:], scalar=1.0, in1=bo_bc[:], op0=ALU.mult, op1=ALU.add,
                    accum_out=z_sum[:, b : b + 1],
                )
                live["z", first + b] = z
            live["z_sum", c] = z_sum

        def mean(c):
            first, count = CHUNKS[c]
            neg_mean = stats.tile([P, 2], F32)
            nc.gpsimd.tensor_scalar(
                out=neg_mean[:, 0:count], in0=live["z_sum", c][:, 0:count], scalar1=-1.0 / ED, scalar2=0.0, op0=ALU.mult, op1=ALU.add
            )
            for b in range(count):
                live["neg_mean", first + b] = neg_mean[:, b : b + 1]

        def variance(c):
            first, count = CHUNKS[c]
            sq_sum = stats.tile([P, 2], F32)
            for b in range(count):
                squares = tiles.tile([P, ED], F32)
                nc.scalar.activation(
                    out=squares[:], in_=live["z", first + b][:], func=ACT.Square, bias=live["neg_mean", first + b],
                    scale=1.0, accum_out=sq_sum[:, b : b + 1],
                )
            rstd = stats.tile([P, 2], F32)
            nc.scalar.activation(
                out=rstd[:, 0:count], in_=sq_sum[:, 0:count], func=ACT.Abs_reciprocal_sqrt, bias=eps[:], scale=1.0 / ED
            )
            for b in range(count):
                live["rstd", first + b] = rstd[:, b : b + 1]
            if shared_norm(first):
                shift = stats.tile([P, 1], F32)
                nc.scalar.activation(out=shift[:], in_=live["neg_mean", first], func=ACT.Copy, scale=live["rstd", first])
                normed = tiles.tile([P, ED], F32)
                nc.scalar.activation(
                    out=normed[:], in_=live["z", first][:], func=ACT.Identity, bias=shift[:], scale=live["rstd", first]
                )
                live["normed", first] = normed

        def shared_norm(r):
            return any(r == first for first, count in CHUNKS[1:3])

        def times_g(r, c):
            if shared_norm(r):
                if c < len(CHUNKS):
                    scaled = live["m", c, 0][:].rearrange("p t e -> p (t e)")[:, 0:ED]
                else:
                    last = tiles.tile([P, ED], F32)
                    scaled = last[:]
                nc.gpsimd.tensor_tensor(out=scaled, in0=live["normed", r][:], in1=g_bc[:], op=ALU.mult)
                live["scaled", r] = scaled

        def centre_times_g(r):
            if shared_norm(r):
                return
            scaled = tiles.tile([P, ED], F32)
            nc.vector.scalar_tensor_tensor(
                out=scaled[:], in0=live["z", r][:], scalar=live["neg_mean", r], in1=g_bc[:], op0=ALU.add, op1=ALU.mult
            )
            live["scaled", r] = scaled

        def residual(r):
            resid = psum_t.tile([P, ED], F32, tag="t")
            nc.tensor.matmul(out=resid[:], lhsT=ident_bf[:], rhs=p_ln_sb[:, r, :], start=True, stop=False)
            nc.tensor.matmul(out=resid[:], lhsT=pick_row[:], rhs=rows[:, 2 * ED : 3 * ED], start=False, stop=True)
            live["resid", r] = resid

        def finish(r):
            result = tiles.tile([P, ED], F32)
            if shared_norm(r):
                nc.vector.tensor_tensor(out=result[:], in0=live["scaled", r], in1=live["resid", r][:], op=ALU.add)
            else:
                nc.vector.scalar_tensor_tensor(
                    out=result[:], in0=live["scaled", r][:], scalar=live["rstd", r], in1=live["resid", r][:], op0=ALU.mult, op1=ALU.add
                )
            nc.sync.dma_start(out=out_rows[:, r, :], in_=result[:])

        def stage(work_of, c, *args):
            if 0 <= c < len(CHUNKS):
                work_of(c, *args)

        def each(work_of, c):
            if 0 <= c < len(CHUNKS):
                for b in range(CHUNKS[c][1]):
                    work_of(CHUNKS[c][0] + b)

        turn_hid(0)
        group_hid(0)
        turn_nodes()
        for h in range(2):
            reorder_scales(h)
        reorder_words(0)
        quantise_hid(0)
        place_x_i(nc.vector, 0, 0)
        first_matmul(0, 0)
        place_x_j(0)
        relu(0, 0)
        reorder_words(1)
        first_matmul(0, 1)
        relu(0, 1)
        turn_p_ln(0)
        for f, b in ((1, 0), (1, 1), (0, 1)):
            place_x_i(nc.gpsimd, f, b)

        for c in range(len(CHUNKS) + 2):
            if c == 0:
                turn_hid(1)
                group_hid(1)
                for n in range(2):
                    spread_ln_row(n)
                place_x_j(1)
            each(residual, c - 2)
            stage(add_x, c)
            if c + 2 < len(CHUNKS):
                place_x_j(c + 2)
            if 0 <= c - 2 < len(CHUNKS):
                times_g(CHUNKS[c - 2][0], c)
            stage(add_bo, c - 1)
            if c == 0:
                stage(add_p_ln, c)
            stage(quantise_hid, c + 1)
            stage(first_matmul, c + 1, 0)
            stage(relu, c + 1, 0)
            if c > 0:
                stage(add_p_ln, c)
            stage(mean, c - 1)
            stage(quantise_s, c)
            if c == 0:
                for n in range(2):
                    copy_ln_row(n)
            each(centre_times_g, c - 1)
            each(finish, c - 2)
            each(second_matmul, c)
            stage(variance, c - 1)
            stage(turn_hid, c + 2)
            stage(group_hid, c + 2)
            stage(first_matmul, c + 1, 1)
            stage(relu, c + 1, 1)
            stage(turn_p_ln, c + 1)
